import numpy as np
import ml_dtypes


def mxq(x, axis, fmt="e4m3"):
    dtype, down = {"e4m3": (ml_dtypes.float8_e4m3fn, 7), "e5m2": (ml_dtypes.float8_e5m2, 14)}[fmt]
    v = np.moveaxis(np.asarray(x, np.float32).astype(ml_dtypes.bfloat16).astype(np.float64), axis, -1)
    blocks = v.reshape(v.shape[:-1] + (-1, 32))
    amax = np.abs(blocks).max(-1, keepdims=True)
    byte = np.maximum(np.where(amax > 0, np.frexp(amax)[1] - 1 + 127, 0) - down, 1)
    scale = np.exp2(byte - 127.0)
    codes = (blocks / scale).astype(np.float32).astype(dtype).astype(np.float64)
    return np.moveaxis((codes * scale).reshape(v.shape), -1, axis)


WIDE = False


def mx_kscale(k):
    if not WIDE:
        return np.ones(k)
    levels = np.array([10, -10, 5, -5, 0])
    a = np.random.permutation(np.resize(levels, k // 512 * 4)).reshape(k // 512, 4)
    idx = np.arange(k)
    return np.exp2(a[idx // 512, idx % 128 // 32])


BF16 = ml_dtypes.bfloat16


def bf(x):
    return np.asarray(x, np.float32).astype(BF16)


def f64(x):
    return np.asarray(x).astype(np.float64)


E2M1 = np.array([0.0, 0.5, 1.0, 1.5, 2.0, 3.0, 4.0, 6.0, -0.0, -0.5, -1.0, -1.5, -2.0, -3.0, -4.0, -6.0])


def pack_weight(w, fmt):
    k, n = w.shape
    w = f64(bf(w)).reshape(k // 32, 32, n)
    amax = np.abs(w).max(1)
    if fmt == "e4m3":
        byte = np.frexp(amax)[1] - 1 + 127 - 7
    else:
        mant, ex = np.frexp(amax / 6.0)
        byte = np.where(mant > 0.5, ex, ex - 1) + 127
    byte = np.clip(np.where(amax > 0, byte, 1), 1, 254)
    scaled = (w * np.exp2(127.0 - byte)[:, None, :]).reshape(k, n).astype(np.float32)
    by_word = np.ascontiguousarray(scaled.reshape(k // 512, 128, 4, n).transpose(0, 1, 3, 2))
    if fmt == "e4m3":
        words = by_word.astype(ml_dtypes.float8_e4m3fn).view(np.uint8)
    else:
        c = by_word.astype(ml_dtypes.float4_e2m1fn).view(np.uint8) & 0xF
        words = c[..., 0::2] | (c[..., 1::2] << 4)
    return np.ascontiguousarray(words), np.ascontiguousarray(byte.astype(np.uint8).reshape(k // 512, 16, n))


def unpack_weight(words, scales, fmt):
    g, p, n, _ = words.shape
    if fmt == "e4m3":
        vals = np.ascontiguousarray(words).view(ml_dtypes.float8_e4m3fn).astype(np.float64)
    else:
        nib = np.empty((g, p, n, 4), np.uint8)
        nib[..., 0::2] = words & 0xF
        nib[..., 1::2] = words >> 4
        vals = E2M1[nib]
    vals = vals * np.repeat(np.exp2(scales.astype(np.float64) - 127.0), 8, axis=1)[..., None]
    return vals.transpose(0, 1, 3, 2).reshape(g * 512, n)


B, S, D_IN, MID, FFN, D_OUT, R = 8, 1024, 256, 512, 512, 256, 16
LN_EPS = 1e-5
FMT = "e4m3"


def silu(v):
    return v / (1.0 + np.exp(-v))


def layer_norm(x, gamma, beta):
    m = np.mean(x, axis=-1, keepdims=True)
    v = np.mean(np.square(x - m), axis=-1, keepdims=True)
    return (x - m) / np.sqrt(v + LN_EPS) * gamma + beta


def setup_inputs():
    t, s = mx_kscale(FFN), mx_kscale(MID)
    h = bf(silu(np.random.standard_normal((B, S, FFN))) * t)
    w_f2 = np.random.standard_normal((MID, FFN)) / np.sqrt(FFN) / t
    b_f2 = bf(0.1 * np.random.standard_normal(MID))
    res1 = bf(0.7 * np.random.standard_normal((B, S, MID)))
    g2 = bf((1.0 + 0.1 * np.random.standard_normal(MID)) * s)
    be2 = bf(0.1 * np.random.standard_normal(MID) * s)
    w_h = np.random.standard_normal((D_OUT, MID)) / np.sqrt(MID) / s
    b_h = bf(0.1 * np.random.standard_normal(D_OUT))
    w_f2_words, w_f2_scales = pack_weight(np.ascontiguousarray(w_f2.T), FMT)
    w_h_words, w_h_scales = pack_weight(np.ascontiguousarray(w_h.T), FMT)
    return {"h": h,
            "w_f2_words": w_f2_words,
            "w_f2_scales": w_f2_scales,
            "b_f2": b_f2,
            "res1": res1,
            "g2": g2,
            "be2": be2,
            "w_h_words": w_h_words,
            "w_h_scales": w_h_scales,
            "b_h": b_h}


def reference(h, w_f2_words, w_f2_scales, b_f2, res1, g2, be2, w_h_words, w_h_scales, b_h):
    ffn = (mxq(f64(h), 2, "e4m3") @ unpack_weight(w_f2_words, w_f2_scales, FMT)) + f64(b_f2)
    res2 = f64(res1) + ffn
    norm2 = layer_norm(res2, f64(g2), f64(be2))
    return (mxq(norm2, 2, "e4m3") @ unpack_weight(w_h_words, w_h_scales, FMT)) + f64(b_h)

@@ -1,0 +1,274 @@
+import concourse.mybir as mybir
+from concourse.masks import make_identity
+
+F32 = mybir.dt.float32
+BF16 = mybir.dt.bfloat16
+I32 = mybir.dt.int32
+U32 = mybir.dt.uint32
+U8 = mybir.dt.uint8
+FP8X4 = mybir.dt.float8_e4m3fn_x4
+ALU = mybir.AluOpType
+ACT = mybir.ActivationFunctionType
+
+P = 128
+PACK = 4
+TOKENS = 8 * 1024
+FFN = 512
+MID = 512
+D_OUT = 256
+LN_EPS = 1e-5
+TILES = 4
+GROUP = P * TILES
+GROUPS = TOKENS // GROUP
+PAIRS = TILES // 2
+
+FLOPS = 2 * TOKENS * (FFN * MID + MID * D_OUT)
+
+
+def load_weight(nc, consts, words_dram, scales_dram, width, name):
+    words = consts.tile([P, width * PACK], U8, name=name + "_words", align_bytes=64)
+    nc.sync.dma_start(
+        out=words[:].bitcast(I32),
+        in_=words_dram[0].rearrange("p n t -> p (n t)").bitcast(I32),
+    )
+    plane = consts.tile([P, width], U8, name=name + "_plane", align_bytes=64)
+    nc.vector.memset(plane[:].bitcast(I32), 0)
+    for r in range(4):
+        nc.sync.dma_start(
+            out=plane[r:P:32, :].bitcast(I32),
+            in_=scales_dram[0, r:16:4, :].bitcast(I32),
+        )
+    return words, plane
+
+
+def tile_tsh_mid_block_pb_t_kernel(
+    tc, h, w_f2_words, w_f2_scales, b_f2, res1, g2, be2, w_h_words, w_h_scales, b_h, out
+):
+    nc = tc.nc
+    h_groups = h.flatten_outer_dims().rearrange("(g p j) k -> g p j k", p=P, j=TILES)
+    res_groups = res1.flatten_outer_dims().rearrange("(g p j) k -> g p j k", p=P, j=TILES)
+    out_groups = out.flatten_outer_dims().rearrange("(g p j) d -> g p j d", p=P, j=TILES)
+
+    with tc.tile_pool(name="consts", bufs=1) as consts, tc.tile_pool(name="loads", bufs=3) as loads, tc.tile_pool(
+        name="work", bufs=2
+    ) as work, tc.tile_pool(name="stats", bufs=3) as stats, tc.psum_pool(
+        name="psum", bufs=1
+    ) as psum, tc.manual_schedule():
+        h_sb, res_sb, hT, h_grouped, h_codes, h_scales, res_bias, ffn = {}, {}, {}, {}, {}, {}, {}, {}
+        x, row_sum, neg_mean, rstd, std, x_hat, xT = {}, {}, {}, {}, {}, {}, {}
+        norm_planes, norm_grouped, norm_codes, norm_scales, head = {}, {}, {}, {}, {}
+
+        def load(g):
+            h_sb[g] = loads.tile([P, TILES, FFN], BF16, name="h_sb")
+            nc.sync.dma_start(out=h_sb[g][:], in_=h_groups[g])
+            res_sb[g] = loads.tile([P, TILES, MID], BF16, name="res_sb")
+            nc.sync.dma_start(out=res_sb[g][:], in_=res_groups[g])
+
+        load(0)
+        wf_words, wf_plane = load_weight(nc, consts, w_f2_words, w_f2_scales, MID, "wf")
+        wh_words, wh_plane = load_weight(nc, consts, w_h_words, w_h_scales, D_OUT, "wh")
+
+        ident = consts.tile([P, P], F32)
+        make_identity(nc, ident[:])
+        eps_col = consts.tile([P, 1], F32)
+        nc.vector.memset(eps_col[:], LN_EPS)
+
+        bf_rows = consts.tile([P, MID], BF16)
+        nc.scalar.dma_start(out=bf_rows[:], in_=b_f2.partition_broadcast(P))
+        bh_rows = consts.tile([P, D_OUT], BF16)
+        nc.scalar.dma_start(out=bh_rows[:], in_=b_h.partition_broadcast(P))
+        gain_bf = consts.tile([P, PACK], BF16)
+        nc.scalar.dma_start(out=gain_bf[:], in_=g2.rearrange("(p t) -> p t", t=PACK))
+        shift_bf = consts.tile([P, PACK], BF16)
+        nc.scalar.dma_start(out=shift_bf[:], in_=be2.rearrange("(p t) -> p t", t=PACK))
+        gain = consts.tile([P, PACK], F32)
+        nc.vector.tensor_copy(out=gain[:], in_=gain_bf[:])
+        shift = consts.tile([P, PACK], F32)
+        nc.vector.tensor_copy(out=shift[:], in_=shift_bf[:])
+
+        def transpose_h(g):
+            h_words = h_sb[g][:].bitcast(F32)
+            for a in range(PAIRS):
+                hT[g, a] = psum.tile([P, 2, 2 * P], F32, name="hT", tag="bank", bufs=6)
+                for jj in range(2):
+                    for u in range(2):
+                        nc.tensor.transpose(
+                            out=hT[g, a][:, u, jj * P : (jj + 1) * P],
+                            in_=h_words[:, 2 * a + jj, u : FFN // 2 : 2],
+                            identity=ident[:],
+                        )
+
+        def copy_h(g, a):
+            if a == 0:
+                h_grouped[g] = work.tile([P, GROUP * PACK], BF16, name="h_grouped", align_bytes=64)
+            words = h_grouped[g][:].bitcast(F32).rearrange("p (c u) -> p c u", u=2)
+            nc.scalar.copy(
+                out=words[:, 2 * a * P : (2 * a + 2) * P, :],
+                in_=hT[g, a][:].rearrange("p u c -> p c u"),
+            )
+
+        def quantise_h(g):
+            h_codes[g] = work.tile([P, GROUP], U32, name="h_codes", align_bytes=64)
+            h_scales[g] = work.tile([P, GROUP], U8, name="h_scales", align_bytes=64)
+            nc.vector.quantize_mx(out=h_codes[g][:].bitcast(FP8X4), scales=h_scales[g][:], in_=h_grouped[g][:])
+
+        def add_bias(g):
+            res_bias[g] = work.tile([P, TILES, MID], F32, name="res_bias")
+            nc.vector.tensor_tensor(
+                out=res_bias[g][:],
+                in0=res_sb[g][:],
+                in1=bf_rows[:].unsqueeze(1).to_broadcast([P, TILES, MID]),
+                op=ALU.add,
+            )
+
+        def first_matmul(g, j):
+            ffn[g, j] = psum.tile([P, MID], F32, name="ffn", tag="ffn", bufs=2)
+            nc.tensor.matmul_mx(
+                out=ffn[g, j][:],
+                lhsT=h_codes[g][:, j * P : (j + 1) * P].bitcast(FP8X4),
+                lhsT_scale=h_scales[g][:, j * P : (j + 1) * P],
+                rhs=wf_words[:].bitcast(FP8X4),
+                rhs_scale=wf_plane[:],
+                start=True,
+                stop=True,
+            )
+
+        def residual_add(g, j):
+            if j == 0:
+                x[g] = work.tile([P, TILES, MID], F32, name="x")
+                row_sum[g] = stats.tile([P, TILES], F32, name="row_sum")
+            nc.vector.scalar_tensor_tensor(
+                out=x[g][:, j, :],
+                in0=ffn[g, j][:],
+                scalar=0.0,
+                in1=res_bias[g][:, j, :],
+                op0=ALU.add,
+                op1=ALU.add,
+                accum_out=row_sum[g][:, j : j + 1],
+            )
+
+        def mean(g):
+            neg_mean[g] = stats.tile([P, TILES], F32, name="neg_mean")
+            nc.vector.tensor_scalar(
+                out=neg_mean[g][:], in0=row_sum[g][:], scalar1=-1.0 / MID, scalar2=None, op0=ALU.mult
+            )
+
+        def deviation(g):
+            sq_sum = stats.tile([P, TILES], F32, name="sq_sum")
+            for j in range(TILES):
+                squares = work.tile([P, MID], BF16, name="squares")
+                nc.scalar.activation(
+                    out=squares[:],
+                    in_=x[g][:, j, :],
+                    func=ACT.Square,
+                    bias=neg_mean[g][:, j : j + 1],
+                    scale=1.0,
+                    accum_out=sq_sum[:, j : j + 1],
+                )
+            std[g] = stats.tile([P, TILES], F32, name="std")
+            nc.scalar.activation(out=std[g][:], in_=sq_sum[:], func=ACT.Sqrt, bias=eps_col[:, 0:1], scale=1.0 / MID)
+
+        def normalise(g):
+            rstd[g] = stats.tile([P, TILES], F32, name="rstd")
+            nc.vector.reciprocal(out=rstd[g][:], in_=std[g][:])
+            x_hat[g] = work.tile([P, TILES, PACK, P], F32, name="x_hat")
+            for j in range(TILES):
+                nc.vector.tensor_scalar(
+                    out=x_hat[g][:, j].rearrange("p t q -> p q t"),
+                    in0=x[g][:, j, :].rearrange("p (q t) -> p q t", t=PACK),
+                    scalar1=neg_mean[g][:, j : j + 1],
+                    scalar2=rstd[g][:, j : j + 1],
+                    op0=ALU.add,
+                    op1=ALU.mult,
+                )
+
+        def transpose_x(g):
+            for t in range(PACK):
+                xT[g, t] = psum.tile([P, GROUP], F32, name="xT", tag="bank", bufs=6)
+            for j in range(TILES):
+                for t in range(PACK):
+                    nc.tensor.transpose(
+                        out=xT[g, t][:, j * P : (j + 1) * P], in_=x_hat[g][:, j, t, :], identity=ident[:]
+                    )
+
+        def gain_shift(g):
+            norm_planes[g] = work.tile([P, PACK, GROUP], BF16, name="norm_planes")
+            for t in range(PACK):
+                nc.scalar.activation(
+                    out=norm_planes[g][:, t, :],
+                    in_=xT[g, t][:],
+                    func=ACT.Identity,
+                    bias=shift[:, t : t + 1],
+                    scale=gain[:, t : t + 1],
+                )
+
+        def regroup(g):
+            norm_grouped[g] = work.tile([P, GROUP, PACK], BF16, name="norm_grouped", align_bytes=64)
+            nc.scalar.copy(
+                out=norm_grouped[g][:].rearrange("p (c i) t -> p c t i", i=4),
+                in_=norm_planes[g][:].rearrange("p t (c i) -> p c t i", i=4),
+            )
+
+        def quantise_norm(g):
+            norm_codes[g] = work.tile([P, GROUP], U32, name="norm_codes", align_bytes=64)
+            norm_scales[g] = work.tile([P, GROUP], U8, name="norm_scales", align_bytes=64)
+            nc.vector.quantize_mx(
+                out=norm_codes[g][:].bitcast(FP8X4),
+                scales=norm_scales[g][:],
+                in_=norm_grouped[g][:].rearrange("p c t -> p (c t)"),
+            )
+
+        def second_matmul(g):
+            for a in range(PAIRS):
+                head[g, a] = psum.tile([P, 2, D_OUT], F32, name="head", tag="bank", bufs=6)
+                for jj in range(2):
+                    j = 2 * a + jj
+                    nc.tensor.matmul_mx(
+                        out=head[g, a][:, jj, :],
+                        lhsT=norm_codes[g][:, j * P : (j + 1) * P].bitcast(FP8X4),
+                        lhsT_scale=norm_scales[g][:, j * P : (j + 1) * P],
+                        rhs=wh_words[:].bitcast(FP8X4),
+                        rhs_scale=wh_plane[:],
+                        start=True,
+                        stop=True,
+                    )
+
+        def finish(g):
+            result = work.tile([P, TILES, D_OUT], F32, name="result")
+            for a in range(PAIRS):
+                nc.vector.tensor_tensor(
+                    out=result[:, 2 * a : 2 * a + 2, :],
+                    in0=head[g, a][:],
+                    in1=bh_rows[:].unsqueeze(1).to_broadcast([P, 2, D_OUT]),
+                    op=ALU.add,
+                )
+            nc.sync.dma_start(out=out_groups[g], in_=result[:])
+
+        def run(stage, g, *which):
+            if 0 <= g < GROUPS:
+                stage(g, *which)
+
+        for i in range(-2, GROUPS + 2):
+            run(load, i + 3)
+            run(quantise_norm, i - 2)
+            run(second_matmul, i - 2)
+            run(gain_shift, i - 1)
+            run(residual_add, i, 0)
+            run(residual_add, i, 1)
+            run(first_matmul, i, 2)
+            run(first_matmul, i, 3)
+            run(residual_add, i, 2)
+            run(residual_add, i, 3)
+            run(mean, i)
+            run(transpose_h, i + 2)
+            run(copy_h, i + 2, 0)
+            run(deviation, i)
+            run(finish, i - 2)
+            run(quantise_h, i + 1)
+            run(first_matmul, i + 1, 0)
+            run(first_matmul, i + 1, 1)
+            run(add_bias, i + 1)
+            run(normalise, i)
+            run(transpose_x, i)
+            run(regroup, i - 1)
+            run(copy_h, i + 2, 1)

@@ -89,7 +89,7 @@ def tile_tsh_mid_block_pb_t_kernel(
         def transpose_h(g):
             h_words = h_sb[g][:].bitcast(F32)
             for a in range(PAIRS):
-                hT[g, a] = psum.tile([P, 2, 2 * P], F32, name="hT", tag="bank", bufs=6)
+                hT[g, a] = psum.tile([P, 2, 2 * P], F32, name="hT", tag="short", bufs=2)
                 for jj in range(2):
                     for u in range(2):
                         nc.tensor.transpose(
@@ -147,13 +147,9 @@ def tile_tsh_mid_block_pb_t_kernel(
                 accum_out=row_sum[g][:, j : j + 1],
             )
 
-        def mean(g):
-            neg_mean[g] = stats.tile([P, TILES], F32, name="neg_mean")
-            nc.vector.tensor_scalar(
-                out=neg_mean[g][:], in0=row_sum[g][:], scalar1=-1.0 / MID, scalar2=None, op0=ALU.mult
-            )
-
         def deviation(g):
+            neg_mean[g] = stats.tile([P, TILES], F32, name="neg_mean")
+            nc.scalar.mul(out=neg_mean[g][:], in_=row_sum[g][:], mul=-1.0 / MID)
             sq_sum = stats.tile([P, TILES], F32, name="sq_sum")
             for j in range(TILES):
                 squares = work.tile([P, MID], BF16, name="squares")
@@ -184,7 +180,7 @@ def tile_tsh_mid_block_pb_t_kernel(
 
         def transpose_x(g):
             for t in range(PACK):
-                xT[g, t] = psum.tile([P, GROUP], F32, name="xT", tag="bank", bufs=6)
+                xT[g, t] = psum.tile([P, GROUP], F32, name="xT", tag="xT", bufs=4)
             for j in range(TILES):
                 for t in range(PACK):
                     nc.tensor.transpose(
@@ -220,7 +216,7 @@ def tile_tsh_mid_block_pb_t_kernel(
 
         def second_matmul(g):
             for a in range(PAIRS):
-                head[g, a] = psum.tile([P, 2, D_OUT], F32, name="head", tag="bank", bufs=6)
+                head[g, a] = psum.tile([P, 2, D_OUT], F32, name="head", tag="short", bufs=2)
                 for jj in range(2):
                     j = 2 * a + jj
                     nc.tensor.matmul_mx(
@@ -248,27 +244,26 @@ def tile_tsh_mid_block_pb_t_kernel(
             if 0 <= g < GROUPS:
                 stage(g, *which)
 
-        for i in range(-2, GROUPS + 2):
-            run(load, i + 3)
-            run(quantise_norm, i - 2)
-            run(second_matmul, i - 2)
-            run(gain_shift, i - 1)
-            run(residual_add, i, 0)
-            run(residual_add, i, 1)
-            run(first_matmul, i, 2)
-            run(first_matmul, i, 3)
-            run(residual_add, i, 2)
-            run(residual_add, i, 3)
-            run(mean, i)
-            run(transpose_h, i + 2)
-            run(copy_h, i + 2, 0)
-            run(deviation, i)
-            run(finish, i - 2)
-            run(quantise_h, i + 1)
-            run(first_matmul, i + 1, 0)
-            run(first_matmul, i + 1, 1)
-            run(add_bias, i + 1)
-            run(normalise, i)
-            run(transpose_x, i)
-            run(regroup, i - 1)
-            run(copy_h, i + 2, 1)
+        for r in range(-2, GROUPS + 2):
+            run(load, r + 3)
+            run(transpose_h, r + 2)
+            run(residual_add, r, 0)
+            run(residual_add, r, 1)
+            run(first_matmul, r, 2)
+            run(first_matmul, r, 3)
+            run(normalise, r - 1)
+            run(transpose_x, r - 1)
+            run(residual_add, r, 2)
+            run(residual_add, r, 3)
+            run(copy_h, r + 2, 0)
+            run(copy_h, r + 2, 1)
+            run(quantise_norm, r - 2)
+            run(second_matmul, r - 2)
+            run(quantise_h, r + 1)
+            run(first_matmul, r + 1, 0)
+            run(first_matmul, r + 1, 1)
+            run(add_bias, r + 1)
+            run(finish, r - 2)
+            run(deviation, r)
+            run(gain_shift, r - 1)
+            run(regroup, r - 1)

@@ -55,7 +55,7 @@ def tile_tsh_mid_block_pb_t_kernel(
         name="psum", bufs=1
     ) as psum, tc.manual_schedule():
         h_sb, res_sb, hT, h_grouped, h_codes, h_scales, res_bias, ffn = {}, {}, {}, {}, {}, {}, {}, {}
-        x, row_sum, neg_mean, rstd, std, x_hat, xT = {}, {}, {}, {}, {}, {}, {}
+        x, row_sum, sq_sum, neg_mean, rstd, std, x_hat, xT = {}, {}, {}, {}, {}, {}, {}, {}
         norm_planes, norm_grouped, norm_codes, norm_scales, head = {}, {}, {}, {}, {}
 
         def load(g):
@@ -147,26 +147,34 @@ def tile_tsh_mid_block_pb_t_kernel(
                 accum_out=row_sum[g][:, j : j + 1],
             )
 
-        def deviation(g):
-            neg_mean[g] = stats.tile([P, TILES], F32, name="neg_mean")
-            nc.scalar.mul(out=neg_mean[g][:], in_=row_sum[g][:], mul=-1.0 / MID)
-            sq_sum = stats.tile([P, TILES], F32, name="sq_sum")
+        def squares(g):
+            sq_sum[g] = stats.tile([P, TILES], F32, name="sq_sum")
             for j in range(TILES):
-                squares = work.tile([P, MID], BF16, name="squares")
+                junk = work.tile([P, MID], BF16, name="junk")
                 nc.scalar.activation(
-                    out=squares[:],
+                    out=junk[:],
                     in_=x[g][:, j, :],
                     func=ACT.Square,
-                    bias=neg_mean[g][:, j : j + 1],
-                    scale=1.0,
-                    accum_out=sq_sum[:, j : j + 1],
+                    bias=row_sum[g][:, j : j + 1],
+                    scale=-float(MID),
+                    accum_out=sq_sum[g][:, j : j + 1],
                 )
-            std[g] = stats.tile([P, TILES], F32, name="std")
-            nc.scalar.activation(out=std[g][:], in_=sq_sum[:], func=ACT.Sqrt, bias=eps_col[:, 0:1], scale=1.0 / MID)
 
-        def normalise(g):
+        def std_dev(g):
+            std[g] = stats.tile([P, TILES], F32, name="std")
+            nc.scalar.activation(
+                out=std[g][:], in_=sq_sum[g][:], func=ACT.Sqrt, bias=eps_col[:, 0:1], scale=1.0 / MID**3
+            )
+
+        def mean(g):
+            neg_mean[g] = stats.tile([P, TILES], F32, name="neg_mean")
+            nc.scalar.mul(out=neg_mean[g][:], in_=row_sum[g][:], mul=-1.0 / MID)
+
+        def inverse_std(g):
             rstd[g] = stats.tile([P, TILES], F32, name="rstd")
             nc.vector.reciprocal(out=rstd[g][:], in_=std[g][:])
+
+        def normalise(g):
             x_hat[g] = work.tile([P, TILES, PACK, P], F32, name="x_hat")
             for j in range(TILES):
                 nc.vector.tensor_scalar(
@@ -187,16 +195,16 @@ def tile_tsh_mid_block_pb_t_kernel(
                         out=xT[g, t][:, j * P : (j + 1) * P], in_=x_hat[g][:, j, t, :], identity=ident[:]
                     )
 
-        def gain_shift(g):
-            norm_planes[g] = work.tile([P, PACK, GROUP], BF16, name="norm_planes")
-            for t in range(PACK):
-                nc.scalar.activation(
-                    out=norm_planes[g][:, t, :],
-                    in_=xT[g, t][:],
-                    func=ACT.Identity,
-                    bias=shift[:, t : t + 1],
-                    scale=gain[:, t : t + 1],
-                )
+        def gain_shift(g, t):
+            if t == 0:
+                norm_planes[g] = work.tile([P, PACK, GROUP], BF16, name="norm_planes")
+            nc.scalar.activation(
+                out=norm_planes[g][:, t, :],
+                in_=xT[g, t][:],
+                func=ACT.Identity,
+                bias=shift[:, t : t + 1],
+                scale=gain[:, t : t + 1],
+            )
 
         def regroup(g):
             norm_grouped[g] = work.tile([P, GROUP, PACK], BF16, name="norm_grouped", align_bytes=64)
@@ -248,6 +256,7 @@ def tile_tsh_mid_block_pb_t_kernel(
             run(load, r + 3)
             run(transpose_h, r + 2)
             run(residual_add, r, 0)
+            run(inverse_std, r - 1)
             run(residual_add, r, 1)
             run(first_matmul, r, 2)
             run(first_matmul, r, 3)
@@ -264,6 +273,11 @@ def tile_tsh_mid_block_pb_t_kernel(
             run(first_matmul, r + 1, 1)
             run(add_bias, r + 1)
             run(finish, r - 2)
-            run(deviation, r)
-            run(gain_shift, r - 1)
+            run(squares, r)
+            run(gain_shift, r - 1, 0)
+            run(std_dev, r)
+            run(gain_shift, r - 1, 1)
+            run(gain_shift, r - 1, 2)
+            run(gain_shift, r - 1, 3)
+            run(mean, r)
             run(regroup, r - 1)

@@ -175,11 +175,11 @@ def tile_tsh_mid_block_pb_t_kernel(
             nc.vector.reciprocal(out=rstd[g][:], in_=std[g][:])
 
         def normalise(g):
-            x_hat[g] = work.tile([P, TILES, PACK, P], F32, name="x_hat")
+            x_hat[g] = work.tile([P, TILES, MID], F32, name="x_hat")
             for j in range(TILES):
                 nc.vector.tensor_scalar(
-                    out=x_hat[g][:, j].rearrange("p t q -> p q t"),
-                    in0=x[g][:, j, :].rearrange("p (q t) -> p q t", t=PACK),
+                    out=x_hat[g][:, j, :],
+                    in0=x[g][:, j, :],
                     scalar1=neg_mean[g][:, j : j + 1],
                     scalar2=rstd[g][:, j : j + 1],
                     op0=ALU.add,
@@ -192,7 +192,7 @@ def tile_tsh_mid_block_pb_t_kernel(
             for j in range(TILES):
                 for t in range(PACK):
                     nc.tensor.transpose(
-                        out=xT[g, t][:, j * P : (j + 1) * P], in_=x_hat[g][:, j, t, :], identity=ident[:]
+                        out=xT[g, t][:, j * P : (j + 1) * P], in_=x_hat[g][:, j, t:MID:PACK], identity=ident[:]
                     )
 
         def gain_shift(g, t):
@@ -246,7 +246,7 @@ def tile_tsh_mid_block_pb_t_kernel(
                     in1=bh_rows[:].unsqueeze(1).to_broadcast([P, 2, D_OUT]),
                     op=ALU.add,
                 )
-            nc.sync.dma_start(out=out_groups[g], in_=result[:])
+                nc.sync.dma_start(out=out_groups[g][:, 2 * a : 2 * a + 2, :], in_=result[:, 2 * a : 2 * a + 2, :])
 
         def run(stage, g, *which):
             if 0 <= g < GROUPS:

@@ -21,6 +21,7 @@ TILES = 4
 GROUP = P * TILES
 GROUPS = TOKENS // GROUP
 PAIRS = TILES // 2
+SCALAR_SHARE = 320
 
 FLOPS = 2 * TOKENS * (FFN * MID + MID * D_OUT)
 
@@ -147,18 +148,18 @@ def tile_tsh_mid_block_pb_t_kernel(
                 accum_out=row_sum[g][:, j : j + 1],
             )
 
-        def squares(g):
-            sq_sum[g] = stats.tile([P, TILES], F32, name="sq_sum")
-            for j in range(TILES):
-                junk = work.tile([P, MID], BF16, name="junk")
-                nc.scalar.activation(
-                    out=junk[:],
-                    in_=x[g][:, j, :],
-                    func=ACT.Square,
-                    bias=row_sum[g][:, j : j + 1],
-                    scale=-float(MID),
-                    accum_out=sq_sum[g][:, j : j + 1],
-                )
+        def squares(g, j):
+            if j == 0:
+                sq_sum[g] = stats.tile([P, TILES], F32, name="sq_sum")
+            junk = work.tile([P, MID], BF16, name="junk")
+            nc.scalar.activation(
+                out=junk[:],
+                in_=x[g][:, j, :],
+                func=ACT.Square,
+                bias=row_sum[g][:, j : j + 1],
+                scale=-float(MID),
+                accum_out=sq_sum[g][:, j : j + 1],
+            )
 
         def std_dev(g):
             std[g] = stats.tile([P, TILES], F32, name="std")
@@ -177,7 +178,7 @@ def tile_tsh_mid_block_pb_t_kernel(
         def normalise(g):
             x_hat[g] = work.tile([P, TILES, MID], F32, name="x_hat")
             for j in range(TILES):
-                nc.vector.tensor_scalar(
+                nc.gpsimd.tensor_scalar(
                     out=x_hat[g][:, j, :],
                     in0=x[g][:, j, :],
                     scalar1=neg_mean[g][:, j : j + 1],
@@ -186,14 +187,14 @@ def tile_tsh_mid_block_pb_t_kernel(
                     op1=ALU.mult,
                 )
 
-        def transpose_x(g):
-            for t in range(PACK):
-                xT[g, t] = psum.tile([P, GROUP], F32, name="xT", tag="xT", bufs=4)
-            for j in range(TILES):
+        def transpose_x(g, j):
+            if j == 0:
                 for t in range(PACK):
-                    nc.tensor.transpose(
-                        out=xT[g, t][:, j * P : (j + 1) * P], in_=x_hat[g][:, j, t:MID:PACK], identity=ident[:]
-                    )
+                    xT[g, t] = psum.tile([P, GROUP], F32, name="xT", tag="xT", bufs=4)
+            for t in range(PACK):
+                nc.tensor.transpose(
+                    out=xT[g, t][:, j * P : (j + 1) * P], in_=x_hat[g][:, j, t:MID:PACK], identity=ident[:]
+                )
 
         def gain_shift(g, t):
             if t == 0:
@@ -206,11 +207,17 @@ def tile_tsh_mid_block_pb_t_kernel(
                 scale=gain[:, t : t + 1],
             )
 
-        def regroup(g):
+        def regroup_on_scalar(g):
             norm_grouped[g] = work.tile([P, GROUP, PACK], BF16, name="norm_grouped", align_bytes=64)
             nc.scalar.copy(
-                out=norm_grouped[g][:].rearrange("p (c i) t -> p c t i", i=4),
-                in_=norm_planes[g][:].rearrange("p t (c i) -> p c t i", i=4),
+                out=norm_grouped[g][:, :SCALAR_SHARE, :].rearrange("p (c i) t -> p c t i", i=4),
+                in_=norm_planes[g][:, :, :SCALAR_SHARE].rearrange("p t (c i) -> p c t i", i=4),
+            )
+
+        def regroup_on_vector(g):
+            nc.vector.tensor_copy(
+                out=norm_grouped[g][:, SCALAR_SHARE:, :].rearrange("p (c i) t -> p c t i", i=4),
+                in_=norm_planes[g][:, :, SCALAR_SHARE:].rearrange("p t (c i) -> p c t i", i=4),
             )
 
         def quantise_norm(g):
@@ -252,32 +259,39 @@ def tile_tsh_mid_block_pb_t_kernel(
             if 0 <= g < GROUPS:
                 stage(g, *which)
 
-        for r in range(-2, GROUPS + 2):
+        for r in range(-2, GROUPS + 3):
             run(load, r + 3)
-            run(transpose_h, r + 2)
-            run(residual_add, r, 0)
             run(inverse_std, r - 1)
+            run(residual_add, r, 0)
             run(residual_add, r, 1)
             run(first_matmul, r, 2)
             run(first_matmul, r, 3)
             run(normalise, r - 1)
-            run(transpose_x, r - 1)
+            run(transpose_x, r - 1, 0)
+            run(transpose_x, r - 1, 1)
+            run(finish, r - 3)
+            run(transpose_h, r + 2)
+            run(transpose_x, r - 1, 2)
+            run(transpose_x, r - 1, 3)
             run(residual_add, r, 2)
             run(residual_add, r, 3)
+            run(squares, r, 0)
+            run(squares, r, 1)
+            run(regroup_on_scalar, r - 2)
+            run(squares, r, 2)
+            run(squares, r, 3)
             run(copy_h, r + 2, 0)
+            run(std_dev, r)
+            run(mean, r)
             run(copy_h, r + 2, 1)
-            run(quantise_norm, r - 2)
-            run(second_matmul, r - 2)
+            run(regroup_on_vector, r - 2)
             run(quantise_h, r + 1)
             run(first_matmul, r + 1, 0)
             run(first_matmul, r + 1, 1)
+            run(quantise_norm, r - 2)
+            run(second_matmul, r - 2)
             run(add_bias, r + 1)
-            run(finish, r - 2)
-            run(squares, r)
             run(gain_shift, r - 1, 0)
-            run(std_dev, r)
             run(gain_shift, r - 1, 1)
             run(gain_shift, r - 1, 2)
             run(gain_shift, r - 1, 3)
-            run(mean, r)
-            run(regroup, r - 1)

@@ -19,9 +19,11 @@ D_OUT = 256
 LN_EPS = 1e-5
 TILES = 4
 GROUP = P * TILES
-GROUPS = TOKENS // GROUP
-PAIRS = TILES // 2
-SCALAR_SHARE = 320
+SIZES = [2] + [TILES] * 15 + [2]
+GROUPS = len(SIZES)
+FIRST_TOKEN = [P * sum(SIZES[:g]) for g in range(GROUPS)]
+assert P * sum(SIZES) == TOKENS
+SCALAR_SHARE = 80
 
 FLOPS = 2 * TOKENS * (FFN * MID + MID * D_OUT)
 
@@ -46,9 +48,19 @@ def tile_tsh_mid_block_pb_t_kernel(
     tc, h, w_f2_words, w_f2_scales, b_f2, res1, g2, be2, w_h_words, w_h_scales, b_h, out
 ):
     nc = tc.nc
-    h_groups = h.flatten_outer_dims().rearrange("(g p j) k -> g p j k", p=P, j=TILES)
-    res_groups = res1.flatten_outer_dims().rearrange("(g p j) k -> g p j k", p=P, j=TILES)
-    out_groups = out.flatten_outer_dims().rearrange("(g p j) d -> g p j d", p=P, j=TILES)
+
+    def by_group(rows):
+        return [
+            rows[FIRST_TOKEN[g] : FIRST_TOKEN[g] + P * SIZES[g], :].rearrange("(p j) k -> p j k", j=SIZES[g])
+            for g in range(GROUPS)
+        ]
+
+    h_groups = by_group(h.flatten_outer_dims())
+    res_groups = by_group(res1.flatten_outer_dims())
+    out_groups = by_group(out.flatten_outer_dims())
+
+    def pairs(g):
+        return [(a, 2 * a, min(2, SIZES[g] - 2 * a)) for a in range((SIZES[g] + 1) // 2)]
 
     with tc.tile_pool(name="consts", bufs=1) as consts, tc.tile_pool(name="loads", bufs=3) as loads, tc.tile_pool(
         name="work", bufs=2
@@ -61,9 +73,9 @@ def tile_tsh_mid_block_pb_t_kernel(
 
         def load(g):
             h_sb[g] = loads.tile([P, TILES, FFN], BF16, name="h_sb")
-            nc.sync.dma_start(out=h_sb[g][:], in_=h_groups[g])
+            nc.sync.dma_start(out=h_sb[g][:, : SIZES[g], :], in_=h_groups[g])
             res_sb[g] = loads.tile([P, TILES, MID], BF16, name="res_sb")
-            nc.sync.dma_start(out=res_sb[g][:], in_=res_groups[g])
+            nc.sync.dma_start(out=res_sb[g][:, : SIZES[g], :], in_=res_groups[g])
 
         load(0)
         wf_words, wf_plane = load_weight(nc, consts, w_f2_words, w_f2_scales, MID, "wf")
@@ -89,36 +101,44 @@ def tile_tsh_mid_block_pb_t_kernel(
 
         def transpose_h(g):
             h_words = h_sb[g][:].bitcast(F32)
-            for a in range(PAIRS):
+            for a, first, count in pairs(g):
                 hT[g, a] = psum.tile([P, 2, 2 * P], F32, name="hT", tag="short", bufs=2)
-                for jj in range(2):
+                for jj in range(count):
                     for u in range(2):
                         nc.tensor.transpose(
                             out=hT[g, a][:, u, jj * P : (jj + 1) * P],
-                            in_=h_words[:, 2 * a + jj, u : FFN // 2 : 2],
+                            in_=h_words[:, first + jj, u : FFN // 2 : 2],
                             identity=ident[:],
                         )
 
         def copy_h(g, a):
             if a == 0:
                 h_grouped[g] = work.tile([P, GROUP * PACK], BF16, name="h_grouped", align_bytes=64)
+            if a >= len(pairs(g)):
+                return
+            first, count = pairs(g)[a][1:]
             words = h_grouped[g][:].bitcast(F32).rearrange("p (c u) -> p c u", u=2)
             nc.scalar.copy(
-                out=words[:, 2 * a * P : (2 * a + 2) * P, :],
-                in_=hT[g, a][:].rearrange("p u c -> p c u"),
+                out=words[:, first * P : (first + count) * P, :],
+                in_=hT[g, a][:, :, : count * P].rearrange("p u c -> p c u"),
             )
 
         def quantise_h(g):
             h_codes[g] = work.tile([P, GROUP], U32, name="h_codes", align_bytes=64)
             h_scales[g] = work.tile([P, GROUP], U8, name="h_scales", align_bytes=64)
-            nc.vector.quantize_mx(out=h_codes[g][:].bitcast(FP8X4), scales=h_scales[g][:], in_=h_grouped[g][:])
+            tokens = P * SIZES[g]
+            nc.vector.quantize_mx(
+                out=h_codes[g][:, :tokens].bitcast(FP8X4),
+                scales=h_scales[g][:, :tokens],
+                in_=h_grouped[g][:, : tokens * PACK],
+            )
 
         def add_bias(g):
             res_bias[g] = work.tile([P, TILES, MID], F32, name="res_bias")
             nc.vector.tensor_tensor(
-                out=res_bias[g][:],
-                in0=res_sb[g][:],
-                in1=bf_rows[:].unsqueeze(1).to_broadcast([P, TILES, MID]),
+                out=res_bias[g][:, : SIZES[g], :],
+                in0=res_sb[g][:, : SIZES[g], :],
+                in1=bf_rows[:].unsqueeze(1).to_broadcast([P, SIZES[g], MID]),
                 op=ALU.add,
             )
 
@@ -162,22 +182,22 @@ def tile_tsh_mid_block_pb_t_kernel(
             )
 
         def std_dev(g):
-            std[g] = stats.tile([P, TILES], F32, name="std")
+            rstd[g] = stats.tile([P, TILES], F32, name="rstd")
             nc.scalar.activation(
-                out=std[g][:], in_=sq_sum[g][:], func=ACT.Sqrt, bias=eps_col[:, 0:1], scale=1.0 / MID**3
+                out=rstd[g][:, : SIZES[g]],
+                in_=sq_sum[g][:, : SIZES[g]],
+                func=ACT.Abs_reciprocal_sqrt,
+                bias=eps_col[:, 0:1],
+                scale=1.0 / MID**3,
             )
 
         def mean(g):
             neg_mean[g] = stats.tile([P, TILES], F32, name="neg_mean")
-            nc.scalar.mul(out=neg_mean[g][:], in_=row_sum[g][:], mul=-1.0 / MID)
-
-        def inverse_std(g):
-            rstd[g] = stats.tile([P, TILES], F32, name="rstd")
-            nc.vector.reciprocal(out=rstd[g][:], in_=std[g][:])
+            nc.scalar.mul(out=neg_mean[g][:, : SIZES[g]], in_=row_sum[g][:, : SIZES[g]], mul=-1.0 / MID)
 
         def normalise(g):
             x_hat[g] = work.tile([P, TILES, MID], F32, name="x_hat")
-            for j in range(TILES):
+            for j in range(SIZES[g]):
                 nc.gpsimd.tensor_scalar(
                     out=x_hat[g][:, j, :],
                     in0=x[g][:, j, :],
@@ -200,8 +220,8 @@ def tile_tsh_mid_block_pb_t_kernel(
             if t == 0:
                 norm_planes[g] = work.tile([P, PACK, GROUP], BF16, name="norm_planes")
             nc.scalar.activation(
-                out=norm_planes[g][:, t, :],
-                in_=xT[g, t][:],
+                out=norm_planes[g][:, t, : P * SIZES[g]],
+                in_=xT[g, t][:, : P * SIZES[g]],
                 func=ACT.Identity,
                 bias=shift[:, t : t + 1],
                 scale=gain[:, t : t + 1],
@@ -209,31 +229,34 @@ def tile_tsh_mid_block_pb_t_kernel(
 
         def regroup_on_scalar(g):
             norm_grouped[g] = work.tile([P, GROUP, PACK], BF16, name="norm_grouped", align_bytes=64)
+            share = SCALAR_SHARE * SIZES[g]
             nc.scalar.copy(
-                out=norm_grouped[g][:, :SCALAR_SHARE, :].rearrange("p (c i) t -> p c t i", i=4),
-                in_=norm_planes[g][:, :, :SCALAR_SHARE].rearrange("p t (c i) -> p c t i", i=4),
+                out=norm_grouped[g][:, :share, :].rearrange("p (c i) t -> p c t i", i=4),
+                in_=norm_planes[g][:, :, :share].rearrange("p t (c i) -> p c t i", i=4),
             )
 
         def regroup_on_vector(g):
+            share, tokens = SCALAR_SHARE * SIZES[g], P * SIZES[g]
             nc.vector.tensor_copy(
-                out=norm_grouped[g][:, SCALAR_SHARE:, :].rearrange("p (c i) t -> p c t i", i=4),
-                in_=norm_planes[g][:, :, SCALAR_SHARE:].rearrange("p t (c i) -> p c t i", i=4),
+                out=norm_grouped[g][:, share:tokens, :].rearrange("p (c i) t -> p c t i", i=4),
+                in_=norm_planes[g][:, :, share:tokens].rearrange("p t (c i) -> p c t i", i=4),
             )
 
         def quantise_norm(g):
             norm_codes[g] = work.tile([P, GROUP], U32, name="norm_codes", align_bytes=64)
             norm_scales[g] = work.tile([P, GROUP], U8, name="norm_scales", align_bytes=64)
+            tokens = P * SIZES[g]
             nc.vector.quantize_mx(
-                out=norm_codes[g][:].bitcast(FP8X4),
-                scales=norm_scales[g][:],
-                in_=norm_grouped[g][:].rearrange("p c t -> p (c t)"),
+                out=norm_codes[g][:, :tokens].bitcast(FP8X4),
+                scales=norm_scales[g][:, :tokens],
+                in_=norm_grouped[g][:, :tokens, :].rearrange("p c t -> p (c t)"),
             )
 
         def second_matmul(g):
-            for a in range(PAIRS):
+            for a, first, count in pairs(g):
                 head[g, a] = psum.tile([P, 2, D_OUT], F32, name="head", tag="short", bufs=2)
-                for jj in range(2):
-                    j = 2 * a + jj
+                for jj in range(count):
+                    j = first + jj
                     nc.tensor.matmul_mx(
                         out=head[g, a][:, jj, :],
                         lhsT=norm_codes[g][:, j * P : (j + 1) * P].bitcast(FP8X4),
@@ -246,22 +269,23 @@ def tile_tsh_mid_block_pb_t_kernel(
 
         def finish(g):
             result = work.tile([P, TILES, D_OUT], F32, name="result")
-            for a in range(PAIRS):
+            for a, first, count in pairs(g):
                 nc.vector.tensor_tensor(
-                    out=result[:, 2 * a : 2 * a + 2, :],
-                    in0=head[g, a][:],
-                    in1=bh_rows[:].unsqueeze(1).to_broadcast([P, 2, D_OUT]),
+                    out=result[:, first : first + count, :],
+                    in0=head[g, a][:, :count, :],
+                    in1=bh_rows[:].unsqueeze(1).to_broadcast([P, count, D_OUT]),
                     op=ALU.add,
                 )
-                nc.sync.dma_start(out=out_groups[g][:, 2 * a : 2 * a + 2, :], in_=result[:, 2 * a : 2 * a + 2, :])
+                nc.sync.dma_start(out=out_groups[g][:, first : first + count, :], in_=result[:, first : first + count, :])
 
         def run(stage, g, *which):
-            if 0 <= g < GROUPS:
+            if 0 <= g < GROUPS and not (stage in by_tile and which[0] >= SIZES[g]):
                 stage(g, *which)
+
+        by_tile = (first_matmul, residual_add, squares, transpose_x)
 
         for r in range(-2, GROUPS + 3):
             run(load, r + 3)
-            run(inverse_std, r - 1)
             run(residual_add, r, 0)
             run(residual_add, r, 1)
             run(first_matmul, r, 2)

@@ -86,18 +86,28 @@ def tile_tsh_mid_block_pb_t_kernel(
         eps_col = consts.tile([P, 1], F32)
         nc.vector.memset(eps_col[:], LN_EPS)
 
+        bias_row = consts.tile([P, MID + D_OUT], BF16)
+        nc.vector.memset(bias_row[:], 0.0)
+        nc.scalar.dma_start(out=bias_row[0:1, :MID], in_=b_f2.unsqueeze(0))
+        nc.scalar.dma_start(out=bias_row[0:1, MID:], in_=b_h.unsqueeze(0))
+        ones = consts.tile([P, P], BF16)
+        nc.vector.memset(ones[:], 1.0)
         bf_rows = consts.tile([P, MID], BF16)
-        nc.scalar.dma_start(out=bf_rows[:], in_=b_f2.partition_broadcast(P))
         bh_rows = consts.tile([P, D_OUT], BF16)
-        nc.scalar.dma_start(out=bh_rows[:], in_=b_h.partition_broadcast(P))
+
+        def spread_biases():
+            for rows, first, width in ((bf_rows, 0, MID), (bh_rows, MID, D_OUT)):
+                bank = psum.tile([P, GROUP], F32, name="bank", tag="xT", bufs=4)
+                nc.tensor.matmul(
+                    out=bank[:, :width], lhsT=ones[:], rhs=bias_row[:, first : first + width], start=True, stop=True
+                )
+                nc.scalar.copy(out=rows[:], in_=bank[:, :width])
         gain_bf = consts.tile([P, PACK], BF16)
         nc.scalar.dma_start(out=gain_bf[:], in_=g2.rearrange("(p t) -> p t", t=PACK))
         shift_bf = consts.tile([P, PACK], BF16)
         nc.scalar.dma_start(out=shift_bf[:], in_=be2.rearrange("(p t) -> p t", t=PACK))
         gain = consts.tile([P, PACK], F32)
-        nc.vector.tensor_copy(out=gain[:], in_=gain_bf[:])
         shift = consts.tile([P, PACK], F32)
-        nc.vector.tensor_copy(out=shift[:], in_=shift_bf[:])
 
         def transpose_h(g):
             h_words = h_sb[g][:].bitcast(F32)
@@ -284,7 +294,22 @@ def tile_tsh_mid_block_pb_t_kernel(
 
         by_tile = (first_matmul, residual_add, squares, transpose_x)
 
-        for r in range(-2, GROUPS + 3):
+        load(1)
+        transpose_h(0)
+        copy_h(0, 0)
+        spread_biases()
+        load(2)
+        quantise_h(0)
+        first_matmul(0, 0)
+        first_matmul(0, 1)
+        add_bias(0)
+        transpose_h(1)
+        copy_h(1, 0)
+        copy_h(1, 1)
+        nc.vector.tensor_copy(out=gain[:], in_=gain_bf[:])
+        nc.vector.tensor_copy(out=shift[:], in_=shift_bf[:])
+
+        for r in range(0, GROUPS + 3):
             run(load, r + 3)
             run(residual_add, r, 0)
             run(residual_add, r, 1)

@@ -71,25 +71,33 @@ def tile_tsh_mid_block_pb_t_kernel(
         x, row_sum, sq_sum, neg_mean, rstd, std, x_hat, xT = {}, {}, {}, {}, {}, {}, {}, {}
         norm_planes, norm_grouped, norm_codes, norm_scales, head = {}, {}, {}, {}, {}
 
-        def load(g):
+        def load_h(g):
             h_sb[g] = loads.tile([P, TILES, FFN], BF16, name="h_sb")
             nc.sync.dma_start(out=h_sb[g][:, : SIZES[g], :], in_=h_groups[g])
+
+        def load_res(g):
             res_sb[g] = loads.tile([P, TILES, MID], BF16, name="res_sb")
             nc.sync.dma_start(out=res_sb[g][:, : SIZES[g], :], in_=res_groups[g])
 
-        load(0)
+        def load(g):
+            load_h(g)
+            load_res(g)
+
+        bias_row = consts.tile([P, MID + D_OUT], BF16)
+        nc.vector.memset(bias_row[:], 0.0)
+        nc.scalar.dma_start(out=bias_row[0:1, :MID], in_=b_f2.unsqueeze(0))
+        nc.scalar.dma_start(out=bias_row[0:1, MID:], in_=b_h.unsqueeze(0))
+
+        load_h(0)
         wf_words, wf_plane = load_weight(nc, consts, w_f2_words, w_f2_scales, MID, "wf")
+        load_res(0)
+        load(1)
         wh_words, wh_plane = load_weight(nc, consts, w_h_words, w_h_scales, D_OUT, "wh")
 
         ident = consts.tile([P, P], F32)
         make_identity(nc, ident[:])
         eps_col = consts.tile([P, 1], F32)
         nc.vector.memset(eps_col[:], LN_EPS)
-
-        bias_row = consts.tile([P, MID + D_OUT], BF16)
-        nc.vector.memset(bias_row[:], 0.0)
-        nc.scalar.dma_start(out=bias_row[0:1, :MID], in_=b_f2.unsqueeze(0))
-        nc.scalar.dma_start(out=bias_row[0:1, MID:], in_=b_h.unsqueeze(0))
         ones = consts.tile([P, P], BF16)
         nc.vector.memset(ones[:], 1.0)
         bf_rows = consts.tile([P, MID], BF16)
@@ -103,9 +111,9 @@ def tile_tsh_mid_block_pb_t_kernel(
                 )
                 nc.scalar.copy(out=rows[:], in_=bank[:, :width])
         gain_bf = consts.tile([P, PACK], BF16)
-        nc.scalar.dma_start(out=gain_bf[:], in_=g2.rearrange("(p t) -> p t", t=PACK))
+        nc.sync.dma_start(out=gain_bf[:], in_=g2.rearrange("(p t) -> p t", t=PACK))
         shift_bf = consts.tile([P, PACK], BF16)
-        nc.scalar.dma_start(out=shift_bf[:], in_=be2.rearrange("(p t) -> p t", t=PACK))
+        nc.sync.dma_start(out=shift_bf[:], in_=be2.rearrange("(p t) -> p t", t=PACK))
         gain = consts.tile([P, PACK], F32)
         shift = consts.tile([P, PACK], F32)
 
@@ -294,11 +302,10 @@ def tile_tsh_mid_block_pb_t_kernel(
 
         by_tile = (first_matmul, residual_add, squares, transpose_x)
 
-        load(1)
+        load(2)
         transpose_h(0)
         copy_h(0, 0)
         spread_biases()
-        load(2)
         quantise_h(0)
         first_matmul(0, 0)
         first_matmul(0, 1)

@@ -344,9 +344,9 @@ def tile_tsh_mid_block_pb_t_kernel(
             run(quantise_h, r + 1)
             run(first_matmul, r + 1, 0)
             run(first_matmul, r + 1, 1)
+            run(add_bias, r + 1)
             run(quantise_norm, r - 2)
             run(second_matmul, r - 2)
-            run(add_bias, r + 1)
             run(gain_shift, r - 1, 0)
             run(gain_shift, r - 1, 1)
             run(gain_shift, r - 1, 2)

@@ -23,7 +23,7 @@ SIZES = [2] + [TILES] * 15 + [2]
 GROUPS = len(SIZES)
 FIRST_TOKEN = [P * sum(SIZES[:g]) for g in range(GROUPS)]
 assert P * sum(SIZES) == TOKENS
-SCALAR_SHARE = 80
+SCALAR_SHARE = 64
 
 FLOPS = 2 * TOKENS * (FFN * MID + MID * D_OUT)
 
@@ -62,9 +62,9 @@ def tile_tsh_mid_block_pb_t_kernel(
     def pairs(g):
         return [(a, 2 * a, min(2, SIZES[g] - 2 * a)) for a in range((SIZES[g] + 1) // 2)]
 
-    with tc.tile_pool(name="consts", bufs=1) as consts, tc.tile_pool(name="loads", bufs=3) as loads, tc.tile_pool(
+    with tc.tile_pool(name="consts", bufs=1) as consts, tc.tile_pool(name="loads", bufs=4) as loads, tc.tile_pool(
         name="work", bufs=2
-    ) as work, tc.tile_pool(name="stats", bufs=3) as stats, tc.psum_pool(
+    ) as work, tc.tile_pool(name="stats", bufs=4) as stats, tc.psum_pool(
         name="psum", bufs=1
     ) as psum, tc.manual_schedule():
         h_sb, res_sb, hT, h_grouped, h_codes, h_scales, res_bias, ffn = {}, {}, {}, {}, {}, {}, {}, {}
@@ -92,7 +92,9 @@ def tile_tsh_mid_block_pb_t_kernel(
         wf_words, wf_plane = load_weight(nc, consts, w_f2_words, w_f2_scales, MID, "wf")
         load_res(0)
         load(1)
+        load_h(2)
         wh_words, wh_plane = load_weight(nc, consts, w_h_words, w_h_scales, D_OUT, "wh")
+        load_res(2)
 
         ident = consts.tile([P, P], F32)
         make_identity(nc, ident[:])
@@ -100,16 +102,15 @@ def tile_tsh_mid_block_pb_t_kernel(
         nc.vector.memset(eps_col[:], LN_EPS)
         ones = consts.tile([P, P], BF16)
         nc.vector.memset(ones[:], 1.0)
-        bf_rows = consts.tile([P, MID], BF16)
         bh_rows = consts.tile([P, D_OUT], BF16)
+        bf_bank = psum.tile([P, MID], F32, name="bf_bank", tag="bf_bank", bufs=1)
 
         def spread_biases():
-            for rows, first, width in ((bf_rows, 0, MID), (bh_rows, MID, D_OUT)):
-                bank = psum.tile([P, GROUP], F32, name="bank", tag="xT", bufs=4)
-                nc.tensor.matmul(
-                    out=bank[:, :width], lhsT=ones[:], rhs=bias_row[:, first : first + width], start=True, stop=True
-                )
-                nc.scalar.copy(out=rows[:], in_=bank[:, :width])
+            nc.tensor.matmul(out=bf_bank[:], lhsT=ones[:], rhs=bias_row[:, :MID], start=True, stop=True)
+            bank = psum.tile([P, GROUP], F32, name="bank", tag="xT", bufs=3)
+            nc.tensor.matmul(out=bank[:, :D_OUT], lhsT=ones[:], rhs=bias_row[:, MID:], start=True, stop=True)
+            nc.scalar.copy(out=bh_rows[:], in_=bank[:, :D_OUT])
+
         gain_bf = consts.tile([P, PACK], BF16)
         nc.sync.dma_start(out=gain_bf[:], in_=g2.rearrange("(p t) -> p t", t=PACK))
         shift_bf = consts.tile([P, PACK], BF16)
@@ -151,13 +152,11 @@ def tile_tsh_mid_block_pb_t_kernel(
                 in_=h_grouped[g][:, : tokens * PACK],
             )
 
-        def add_bias(g):
-            res_bias[g] = work.tile([P, TILES, MID], F32, name="res_bias")
+        def add_bias(g, j):
+            if j == 0:
+                res_bias[g] = work.tile([P, TILES, MID], F32, name="res_bias")
             nc.vector.tensor_tensor(
-                out=res_bias[g][:, : SIZES[g], :],
-                in0=res_sb[g][:, : SIZES[g], :],
-                in1=bf_rows[:].unsqueeze(1).to_broadcast([P, SIZES[g], MID]),
-                op=ALU.add,
+                out=res_bias[g][:, j, :], in0=res_sb[g][:, j, :], in1=bf_bank[:], op=ALU.add
             )
 
         def first_matmul(g, j):
@@ -174,7 +173,7 @@ def tile_tsh_mid_block_pb_t_kernel(
 
         def residual_add(g, j):
             if j == 0:
-                x[g] = work.tile([P, TILES, MID], F32, name="x")
+                x[g] = work.tile([P, TILES, MID], F32, name="x", bufs=3)
                 row_sum[g] = stats.tile([P, TILES], F32, name="row_sum")
             nc.vector.scalar_tensor_tensor(
                 out=x[g][:, j, :],
@@ -225,18 +224,16 @@ def tile_tsh_mid_block_pb_t_kernel(
                     op1=ALU.mult,
                 )
 
-        def transpose_x(g, j):
-            if j == 0:
-                for t in range(PACK):
-                    xT[g, t] = psum.tile([P, GROUP], F32, name="xT", tag="xT", bufs=4)
-            for t in range(PACK):
+        def transpose_x(g, t):
+            xT[g, t] = psum.tile([P, GROUP], F32, name="xT", tag="xT", bufs=3)
+            for j in range(SIZES[g]):
                 nc.tensor.transpose(
                     out=xT[g, t][:, j * P : (j + 1) * P], in_=x_hat[g][:, j, t:MID:PACK], identity=ident[:]
                 )
 
         def gain_shift(g, t):
             if t == 0:
-                norm_planes[g] = work.tile([P, PACK, GROUP], BF16, name="norm_planes")
+                norm_planes[g] = work.tile([P, PACK, GROUP], BF16, name="norm_planes", bufs=3)
             nc.scalar.activation(
                 out=norm_planes[g][:, t, : P * SIZES[g]],
                 in_=xT[g, t][:, : P * SIZES[g]],
@@ -253,11 +250,15 @@ def tile_tsh_mid_block_pb_t_kernel(
                 in_=norm_planes[g][:, :, :share].rearrange("p t (c i) -> p c t i", i=4),
             )
 
-        def regroup_on_vector(g):
+        def regroup_on_gpsimd(g):
             share, tokens = SCALAR_SHARE * SIZES[g], P * SIZES[g]
-            nc.vector.tensor_copy(
-                out=norm_grouped[g][:, share:tokens, :].rearrange("p (c i) t -> p c t i", i=4),
-                in_=norm_planes[g][:, :, share:tokens].rearrange("p t (c i) -> p c t i", i=4),
+            nc.gpsimd.tensor_scalar(
+                out=norm_grouped[g][:, share:tokens, :],
+                in0=norm_planes[g][:, :, share:tokens].rearrange("p t n -> p n t"),
+                scalar1=1.0,
+                scalar2=0.0,
+                op0=ALU.mult,
+                op1=ALU.add,
             )
 
         def quantise_norm(g):
@@ -300,54 +301,56 @@ def tile_tsh_mid_block_pb_t_kernel(
             if 0 <= g < GROUPS and not (stage in by_tile and which[0] >= SIZES[g]):
                 stage(g, *which)
 
-        by_tile = (first_matmul, residual_add, squares, transpose_x)
+        by_tile = (first_matmul, residual_add, squares, add_bias)
 
-        load(2)
+        load(3)
         transpose_h(0)
         copy_h(0, 0)
         spread_biases()
         quantise_h(0)
         first_matmul(0, 0)
         first_matmul(0, 1)
-        add_bias(0)
+        add_bias(0, 0)
+        add_bias(0, 1)
         transpose_h(1)
-        copy_h(1, 0)
-        copy_h(1, 1)
-        nc.vector.tensor_copy(out=gain[:], in_=gain_bf[:])
-        nc.vector.tensor_copy(out=shift[:], in_=shift_bf[:])
+        nc.gpsimd.tensor_copy(out=gain[:], in_=gain_bf[:])
+        nc.gpsimd.tensor_copy(out=shift[:], in_=shift_bf[:])
 
         for r in range(0, GROUPS + 3):
-            run(load, r + 3)
+            run(load, r + 4)
             run(residual_add, r, 0)
+            run(add_bias, r + 1, 0)
+            run(copy_h, r + 1, 0)
+            run(copy_h, r + 1, 1)
+            run(transpose_x, r - 2, 0)
+            run(transpose_x, r - 2, 1)
+            run(transpose_x, r - 2, 2)
             run(residual_add, r, 1)
+            run(add_bias, r + 1, 1)
+            run(gain_shift, r - 2, 0)
             run(first_matmul, r, 2)
             run(first_matmul, r, 3)
-            run(normalise, r - 1)
-            run(transpose_x, r - 1, 0)
-            run(transpose_x, r - 1, 1)
-            run(finish, r - 3)
-            run(transpose_h, r + 2)
-            run(transpose_x, r - 1, 2)
-            run(transpose_x, r - 1, 3)
+            run(transpose_x, r - 2, 3)
+            run(gain_shift, r - 2, 1)
+            run(std_dev, r - 1)
+            run(mean, r - 1)
+            run(gain_shift, r - 2, 2)
+            run(gain_shift, r - 2, 3)
+            run(quantise_norm, r - 3)
+            run(quantise_h, r + 1)
+            run(second_matmul, r - 3)
             run(residual_add, r, 2)
+            run(add_bias, r + 1, 2)
+            run(first_matmul, r + 1, 0)
             run(residual_add, r, 3)
+            run(add_bias, r + 1, 3)
+            run(first_matmul, r + 1, 1)
             run(squares, r, 0)
             run(squares, r, 1)
             run(regroup_on_scalar, r - 2)
             run(squares, r, 2)
             run(squares, r, 3)
-            run(copy_h, r + 2, 0)
-            run(std_dev, r)
-            run(mean, r)
-            run(copy_h, r + 2, 1)
-            run(regroup_on_vector, r - 2)
-            run(quantise_h, r + 1)
-            run(first_matmul, r + 1, 0)
-            run(first_matmul, r + 1, 1)
-            run(add_bias, r + 1)
-            run(quantise_norm, r - 2)
-            run(second_matmul, r - 2)
-            run(gain_shift, r - 1, 0)
-            run(gain_shift, r - 1, 1)
-            run(gain_shift, r - 1, 2)
-            run(gain_shift, r - 1, 3)
+            run(normalise, r - 1)
+            run(regroup_on_gpsimd, r - 2)
+            run(finish, r - 3)
+            run(transpose_h, r + 2)

@@ -89,8 +89,8 @@ def tile_tsh_mid_block_pb_t_kernel(
         nc.scalar.dma_start(out=bias_row[0:1, MID:], in_=b_h.unsqueeze(0))
 
         load_h(0)
-        wf_words, wf_plane = load_weight(nc, consts, w_f2_words, w_f2_scales, MID, "wf")
         load_res(0)
+        wf_words, wf_plane = load_weight(nc, consts, w_f2_words, w_f2_scales, MID, "wf")
         load(1)
         load_h(2)
         wh_words, wh_plane = load_weight(nc, consts, w_h_words, w_h_scales, D_OUT, "wh")
@@ -212,10 +212,10 @@ def tile_tsh_mid_block_pb_t_kernel(
             neg_mean[g] = stats.tile([P, TILES], F32, name="neg_mean")
             nc.scalar.mul(out=neg_mean[g][:, : SIZES[g]], in_=row_sum[g][:, : SIZES[g]], mul=-1.0 / MID)
 
-        def normalise(g):
+        def normalise(g, engine=nc.gpsimd):
             x_hat[g] = work.tile([P, TILES, MID], F32, name="x_hat")
             for j in range(SIZES[g]):
-                nc.gpsimd.tensor_scalar(
+                engine.tensor_scalar(
                     out=x_hat[g][:, j, :],
                     in0=x[g][:, j, :],
                     scalar1=neg_mean[g][:, j : j + 1],
@@ -225,7 +225,11 @@ def tile_tsh_mid_block_pb_t_kernel(
                 )
 
         def transpose_x(g, t):
-            xT[g, t] = psum.tile([P, GROUP], F32, name="xT", tag="xT", bufs=3)
+            if g < GROUPS - 1:
+                xT[g, t] = psum.tile([P, GROUP], F32, name="xT", tag="xT", bufs=3)
+            elif t % 2 == 0:
+                both = psum.tile([P, GROUP], F32, name="both", tag="ffn", bufs=2)
+                xT[g, t], xT[g, t + 1] = both[:, : GROUP // 2], both[:, GROUP // 2 :]
             for j in range(SIZES[g]):
                 nc.tensor.transpose(
                     out=xT[g, t][:, j * P : (j + 1) * P], in_=x_hat[g][:, j, t:MID:PACK], identity=ident[:]
@@ -261,6 +265,14 @@ def tile_tsh_mid_block_pb_t_kernel(
                 op1=ALU.add,
             )
 
+        def regroup_alone(g, copy):
+            tokens = P * SIZES[g]
+            norm_grouped[g] = work.tile([P, GROUP, PACK], BF16, name="norm_grouped", align_bytes=64)
+            copy(
+                out=norm_grouped[g][:, :tokens, :].rearrange("p (c i) t -> p c t i", i=4),
+                in_=norm_planes[g][:, :, :tokens].rearrange("p t (c i) -> p c t i", i=4),
+            )
+
         def quantise_norm(g):
             norm_codes[g] = work.tile([P, GROUP], U32, name="norm_codes", align_bytes=64)
             norm_scales[g] = work.tile([P, GROUP], U8, name="norm_scales", align_bytes=64)
@@ -287,7 +299,7 @@ def tile_tsh_mid_block_pb_t_kernel(
                     )
 
         def finish(g):
-            result = work.tile([P, TILES, D_OUT], F32, name="result")
+            result = work.tile([P, TILES, D_OUT], F32, name="result", bufs=3)
             for a, first, count in pairs(g):
                 nc.vector.tensor_tensor(
                     out=result[:, first : first + count, :],
@@ -307,16 +319,17 @@ def tile_tsh_mid_block_pb_t_kernel(
         transpose_h(0)
         copy_h(0, 0)
         spread_biases()
+        add_bias(0, 0)
+        add_bias(0, 1)
         quantise_h(0)
         first_matmul(0, 0)
         first_matmul(0, 1)
-        add_bias(0, 0)
-        add_bias(0, 1)
         transpose_h(1)
         nc.gpsimd.tensor_copy(out=gain[:], in_=gain_bf[:])
         nc.gpsimd.tensor_copy(out=shift[:], in_=shift_bf[:])
 
-        for r in range(0, GROUPS + 3):
+        LAST = GROUPS - 1
+        for r in range(LAST):
             run(load, r + 4)
             run(residual_add, r, 0)
             run(add_bias, r + 1, 0)
@@ -347,10 +360,59 @@ def tile_tsh_mid_block_pb_t_kernel(
             run(first_matmul, r + 1, 1)
             run(squares, r, 0)
             run(squares, r, 1)
-            run(regroup_on_scalar, r - 2)
+            if r < LAST - 1:
+                run(regroup_on_scalar, r - 2)
             run(squares, r, 2)
             run(squares, r, 3)
             run(normalise, r - 1)
-            run(regroup_on_gpsimd, r - 2)
+            if r < LAST - 1:
+                run(regroup_on_gpsimd, r - 2)
             run(finish, r - 3)
             run(transpose_h, r + 2)
+
+        residual_add(LAST, 0)
+        residual_add(LAST, 1)
+        regroup_alone(LAST - 3, nc.vector.tensor_copy)
+        quantise_norm(LAST - 3)
+        std_dev(LAST - 1)
+        mean(LAST - 1)
+        squares(LAST, 0)
+        squares(LAST, 1)
+        std_dev(LAST)
+        mean(LAST)
+        transpose_x(LAST - 2, 0)
+        transpose_x(LAST - 2, 1)
+        transpose_x(LAST - 2, 2)
+        normalise(LAST - 1, nc.vector)
+        normalise(LAST, nc.vector)
+        gain_shift(LAST - 2, 0)
+        transpose_x(LAST - 2, 3)
+        second_matmul(LAST - 3)
+        gain_shift(LAST - 2, 1)
+        transpose_x(LAST - 1, 0)
+        gain_shift(LAST - 2, 2)
+        transpose_x(LAST - 1, 1)
+        gain_shift(LAST - 2, 3)
+        transpose_x(LAST - 1, 2)
+        finish(LAST - 3)
+        regroup_alone(LAST - 2, nc.vector.tensor_copy)
+        quantise_norm(LAST - 2)
+        gain_shift(LAST - 1, 0)
+        transpose_x(LAST - 1, 3)
+        for t in range(PACK):
+            transpose_x(LAST, t)
+        second_matmul(LAST - 2)
+        gain_shift(LAST - 1, 1)
+        gain_shift(LAST - 1, 2)
+        gain_shift(LAST - 1, 3)
+        regroup_alone(LAST - 1, nc.vector.tensor_copy)
+        quantise_norm(LAST - 1)
+        for t in range(PACK):
+            gain_shift(LAST, t)
+        finish(LAST - 2)
+        second_matmul(LAST - 1)
+        regroup_alone(LAST, nc.scalar.copy)
+        quantise_norm(LAST)
+        finish(LAST - 1)
+        second_matmul(LAST)
+        finish(LAST)

@@ -62,7 +62,7 @@ def tile_tsh_mid_block_pb_t_kernel(
     def pairs(g):
         return [(a, 2 * a, min(2, SIZES[g] - 2 * a)) for a in range((SIZES[g] + 1) // 2)]
 
-    with tc.tile_pool(name="consts", bufs=1) as consts, tc.tile_pool(name="loads", bufs=4) as loads, tc.tile_pool(
+    with tc.tile_pool(name="consts", bufs=1) as consts, tc.tile_pool(name="loads", bufs=5) as loads, tc.tile_pool(
         name="work", bufs=2
     ) as work, tc.tile_pool(name="stats", bufs=4) as stats, tc.psum_pool(
         name="psum", bufs=1
@@ -83,6 +83,11 @@ def tile_tsh_mid_block_pb_t_kernel(
             load_h(g)
             load_res(g)
 
+        eps_col = consts.tile([P, 1], F32)
+        nc.vector.memset(eps_col[:], LN_EPS)
+        warm = consts.tile([P, 1], F32)
+        nc.scalar.activation(out=warm[:], in_=eps_col[:], func=ACT.Abs_reciprocal_sqrt)
+
         bias_row = consts.tile([P, MID + D_OUT], BF16)
         nc.vector.memset(bias_row[:], 0.0)
         nc.scalar.dma_start(out=bias_row[0:1, :MID], in_=b_f2.unsqueeze(0))
@@ -98,8 +103,6 @@ def tile_tsh_mid_block_pb_t_kernel(
 
         ident = consts.tile([P, P], F32)
         make_identity(nc, ident[:])
-        eps_col = consts.tile([P, 1], F32)
-        nc.vector.memset(eps_col[:], LN_EPS)
         ones = consts.tile([P, P], BF16)
         nc.vector.memset(ones[:], 1.0)
         bh_rows = consts.tile([P, D_OUT], BF16)
@@ -152,11 +155,17 @@ def tile_tsh_mid_block_pb_t_kernel(
                 in_=h_grouped[g][:, : tokens * PACK],
             )
 
-        def add_bias(g, j):
-            if j == 0:
+        def add_bias(g, a):
+            if a == 0:
                 res_bias[g] = work.tile([P, TILES, MID], F32, name="res_bias")
+            if a >= len(pairs(g)):
+                return
+            first, count = pairs(g)[a][1:]
             nc.vector.tensor_tensor(
-                out=res_bias[g][:, j, :], in0=res_sb[g][:, j, :], in1=bf_bank[:], op=ALU.add
+                out=res_bias[g][:, first : first + count, :],
+                in0=res_sb[g][:, first : first + count, :],
+                in1=bf_bank[:].unsqueeze(1).to_broadcast([P, count, MID]),
+                op=ALU.add,
             )
 
         def first_matmul(g, j):
@@ -213,7 +222,7 @@ def tile_tsh_mid_block_pb_t_kernel(
             nc.scalar.mul(out=neg_mean[g][:, : SIZES[g]], in_=row_sum[g][:, : SIZES[g]], mul=-1.0 / MID)
 
         def normalise(g, engine=nc.gpsimd):
-            x_hat[g] = work.tile([P, TILES, MID], F32, name="x_hat")
+            x_hat[g] = work.tile([P, TILES, MID], F32, name="x_hat", bufs=3)
             for j in range(SIZES[g]):
                 engine.tensor_scalar(
                     out=x_hat[g][:, j, :],
@@ -313,33 +322,41 @@ def tile_tsh_mid_block_pb_t_kernel(
             if 0 <= g < GROUPS and not (stage in by_tile and which[0] >= SIZES[g]):
                 stage(g, *which)
 
-        by_tile = (first_matmul, residual_add, squares, add_bias)
+        by_tile = (first_matmul, residual_add, squares)
 
         load(3)
+        load(4)
         transpose_h(0)
         copy_h(0, 0)
         spread_biases()
-        add_bias(0, 0)
-        add_bias(0, 1)
         quantise_h(0)
+        add_bias(0, 0)
         first_matmul(0, 0)
         first_matmul(0, 1)
         transpose_h(1)
+        copy_h(1, 0)
+        copy_h(1, 1)
+        transpose_h(2)
+        residual_add(0, 0)
+        residual_add(0, 1)
+        squares(0, 0)
+        squares(0, 1)
         nc.gpsimd.tensor_copy(out=gain[:], in_=gain_bf[:])
         nc.gpsimd.tensor_copy(out=shift[:], in_=shift_bf[:])
 
         LAST = GROUPS - 1
         for r in range(LAST):
-            run(load, r + 4)
-            run(residual_add, r, 0)
+            run(load, r + 5)
+            if r > 0:
+                run(residual_add, r, 0)
             run(add_bias, r + 1, 0)
-            run(copy_h, r + 1, 0)
-            run(copy_h, r + 1, 1)
+            run(copy_h, r + 2, 0)
+            run(copy_h, r + 2, 1)
             run(transpose_x, r - 2, 0)
             run(transpose_x, r - 2, 1)
             run(transpose_x, r - 2, 2)
-            run(residual_add, r, 1)
-            run(add_bias, r + 1, 1)
+            if r > 0:
+                run(residual_add, r, 1)
             run(gain_shift, r - 2, 0)
             run(first_matmul, r, 2)
             run(first_matmul, r, 3)
@@ -348,18 +365,19 @@ def tile_tsh_mid_block_pb_t_kernel(
             run(std_dev, r - 1)
             run(mean, r - 1)
             run(gain_shift, r - 2, 2)
+            if r > 0:
+                run(squares, r, 0)
             run(gain_shift, r - 2, 3)
             run(quantise_norm, r - 3)
             run(quantise_h, r + 1)
             run(second_matmul, r - 3)
             run(residual_add, r, 2)
-            run(add_bias, r + 1, 2)
+            run(add_bias, r + 1, 1)
             run(first_matmul, r + 1, 0)
             run(residual_add, r, 3)
-            run(add_bias, r + 1, 3)
             run(first_matmul, r + 1, 1)
-            run(squares, r, 0)
-            run(squares, r, 1)
+            if r > 0:
+                run(squares, r, 1)
             if r < LAST - 1:
                 run(regroup_on_scalar, r - 2)
             run(squares, r, 2)
@@ -368,7 +386,7 @@ def tile_tsh_mid_block_pb_t_kernel(
             if r < LAST - 1:
                 run(regroup_on_gpsimd, r - 2)
             run(finish, r - 3)
-            run(transpose_h, r + 2)
+            run(transpose_h, r + 3)
 
         residual_add(LAST, 0)
         residual_add(LAST, 1)

@@ -25,6 +25,8 @@ FIRST_TOKEN = [P * sum(SIZES[:g]) for g in range(GROUPS)]
 assert P * sum(SIZES) == TOKENS
 SCALAR_SHARE = 64
 
+GPSIMD_ADDS = [0, 2, 1, 0] + [0] * (GROUPS - 4)
+
 FLOPS = 2 * TOKENS * (FFN * MID + MID * D_OUT)
 
 
@@ -67,9 +69,9 @@ def tile_tsh_mid_block_pb_t_kernel(
     ) as work, tc.tile_pool(name="stats", bufs=4) as stats, tc.psum_pool(
         name="psum", bufs=1
     ) as psum, tc.manual_schedule():
-        h_sb, res_sb, hT, h_grouped, h_codes, h_scales, res_bias, ffn = {}, {}, {}, {}, {}, {}, {}, {}
+        h_sb, res_sb, hT, grouped, codes, scales, res_bias, ffn = {}, {}, {}, {}, {}, {}, {}, {}
         x, row_sum, sq_sum, neg_mean, rstd, std, x_hat, xT = {}, {}, {}, {}, {}, {}, {}, {}
-        norm_planes, norm_grouped, norm_codes, norm_scales, head = {}, {}, {}, {}, {}
+        norm_planes, head = {}, {}
 
         def load_h(g):
             h_sb[g] = loads.tile([P, TILES, FFN], BF16, name="h_sb")
@@ -105,6 +107,7 @@ def tile_tsh_mid_block_pb_t_kernel(
         make_identity(nc, ident[:])
         ones = consts.tile([P, P], BF16)
         nc.vector.memset(ones[:], 1.0)
+        bf_rows = consts.tile([P, MID], BF16)
         bh_rows = consts.tile([P, D_OUT], BF16)
         bf_bank = psum.tile([P, MID], F32, name="bf_bank", tag="bf_bank", bufs=1)
 
@@ -113,6 +116,7 @@ def tile_tsh_mid_block_pb_t_kernel(
             bank = psum.tile([P, GROUP], F32, name="bank", tag="xT", bufs=3)
             nc.tensor.matmul(out=bank[:, :D_OUT], lhsT=ones[:], rhs=bias_row[:, MID:], start=True, stop=True)
             nc.scalar.copy(out=bh_rows[:], in_=bank[:, :D_OUT])
+            nc.scalar.copy(out=bf_rows[:], in_=bf_bank[:])
 
         gain_bf = consts.tile([P, PACK], BF16)
         nc.sync.dma_start(out=gain_bf[:], in_=g2.rearrange("(p t) -> p t", t=PACK))
@@ -133,34 +137,42 @@ def tile_tsh_mid_block_pb_t_kernel(
                             identity=ident[:],
                         )
 
+        def joint(c):
+            if c not in grouped:
+                grouped[c] = work.tile([P, 2 * GROUP, PACK], BF16, name="grouped", align_bytes=64, bufs=4)
+            return grouped[c]
+
         def copy_h(g, a):
-            if a == 0:
-                h_grouped[g] = work.tile([P, GROUP * PACK], BF16, name="h_grouped", align_bytes=64)
             if a >= len(pairs(g)):
                 return
             first, count = pairs(g)[a][1:]
-            words = h_grouped[g][:].bitcast(F32).rearrange("p (c u) -> p c u", u=2)
+            words = joint(g - 1)[:, GROUP:, :].rearrange("p c t -> p (c t)").bitcast(F32).rearrange("p (c u) -> p c u", u=2)
             nc.scalar.copy(
                 out=words[:, first * P : (first + count) * P, :],
                 in_=hT[g, a][:, :, : count * P].rearrange("p u c -> p c u"),
             )
 
-        def quantise_h(g):
-            h_codes[g] = work.tile([P, GROUP], U32, name="h_codes", align_bytes=64)
-            h_scales[g] = work.tile([P, GROUP], U8, name="h_scales", align_bytes=64)
-            tokens = P * SIZES[g]
-            nc.vector.quantize_mx(
-                out=h_codes[g][:, :tokens].bitcast(FP8X4),
-                scales=h_scales[g][:, :tokens],
-                in_=h_grouped[g][:, : tokens * PACK],
-            )
+        def quantise(c):
+            codes[c] = work.tile([P, 2 * GROUP], U32, name="codes", align_bytes=64, bufs=4)
+            scales[c] = work.tile([P, 2 * GROUP], U8, name="scales", align_bytes=64, bufs=4)
+            norm = P * SIZES[c - 3] if 0 <= c - 3 < GROUPS else 0
+            h_end = GROUP + (P * SIZES[c + 1] if c + 1 < GROUPS else 0)
+            spans = [(0, 2 * GROUP)] if (norm, h_end) == (GROUP, 2 * GROUP) else [(0, norm), (GROUP, h_end)]
+            for lo, hi in spans:
+                if lo < hi:
+                    nc.vector.quantize_mx(
+                        out=codes[c][:, lo:hi].bitcast(FP8X4),
+                        scales=scales[c][:, lo:hi],
+                        in_=grouped[c][:, lo:hi, :].rearrange("p c t -> p (c t)"),
+                    )
 
         def add_bias(g, a):
             if a == 0:
                 res_bias[g] = work.tile([P, TILES, MID], F32, name="res_bias")
-            if a >= len(pairs(g)):
+            first = 2 * a
+            count = min(first + 2, SIZES[g] - GPSIMD_ADDS[g]) - first
+            if count <= 0:
                 return
-            first, count = pairs(g)[a][1:]
             nc.vector.tensor_tensor(
                 out=res_bias[g][:, first : first + count, :],
                 in0=res_sb[g][:, first : first + count, :],
@@ -168,12 +180,18 @@ def tile_tsh_mid_block_pb_t_kernel(
                 op=ALU.add,
             )
 
+        def add_bias_on_gpsimd(g):
+            for j in range(SIZES[g] - GPSIMD_ADDS[g], SIZES[g]):
+                nc.gpsimd.tensor_tensor(
+                    out=res_bias[g][:, j, :], in0=res_sb[g][:, j, :], in1=bf_rows[:], op=ALU.add
+                )
+
         def first_matmul(g, j):
             ffn[g, j] = psum.tile([P, MID], F32, name="ffn", tag="ffn", bufs=2)
             nc.tensor.matmul_mx(
                 out=ffn[g, j][:],
-                lhsT=h_codes[g][:, j * P : (j + 1) * P].bitcast(FP8X4),
-                lhsT_scale=h_scales[g][:, j * P : (j + 1) * P],
+                lhsT=codes[g - 1][:, GROUP + j * P : GROUP + (j + 1) * P].bitcast(FP8X4),
+                lhsT_scale=scales[g - 1][:, GROUP + j * P : GROUP + (j + 1) * P],
                 rhs=wf_words[:].bitcast(FP8X4),
                 rhs_scale=wf_plane[:],
                 start=True,
@@ -234,10 +252,12 @@ def tile_tsh_mid_block_pb_t_kernel(
                 )
 
         def transpose_x(g, t):
-            if g < GROUPS - 1:
+            if g == GROUPS - 2 and t < 2:
+                xT[g, t] = psum.tile([P, GROUP], F32, name="xT_late", tag="ffn", bufs=2)
+            elif g < GROUPS - 1:
                 xT[g, t] = psum.tile([P, GROUP], F32, name="xT", tag="xT", bufs=3)
             elif t % 2 == 0:
-                both = psum.tile([P, GROUP], F32, name="both", tag="ffn", bufs=2)
+                both = psum.tile([P, GROUP], F32, name="both", tag="xT", bufs=3)
                 xT[g, t], xT[g, t + 1] = both[:, : GROUP // 2], both[:, GROUP // 2 :]
             for j in range(SIZES[g]):
                 nc.tensor.transpose(
@@ -256,17 +276,16 @@ def tile_tsh_mid_block_pb_t_kernel(
             )
 
         def regroup_on_scalar(g):
-            norm_grouped[g] = work.tile([P, GROUP, PACK], BF16, name="norm_grouped", align_bytes=64)
             share = SCALAR_SHARE * SIZES[g]
             nc.scalar.copy(
-                out=norm_grouped[g][:, :share, :].rearrange("p (c i) t -> p c t i", i=4),
+                out=joint(g + 3)[:, :share, :].rearrange("p (c i) t -> p c t i", i=4),
                 in_=norm_planes[g][:, :, :share].rearrange("p t (c i) -> p c t i", i=4),
             )
 
         def regroup_on_gpsimd(g):
             share, tokens = SCALAR_SHARE * SIZES[g], P * SIZES[g]
             nc.gpsimd.tensor_scalar(
-                out=norm_grouped[g][:, share:tokens, :],
+                out=joint(g + 3)[:, share:tokens, :],
                 in0=norm_planes[g][:, :, share:tokens].rearrange("p t n -> p n t"),
                 scalar1=1.0,
                 scalar2=0.0,
@@ -276,20 +295,9 @@ def tile_tsh_mid_block_pb_t_kernel(
 
         def regroup_alone(g, copy):
             tokens = P * SIZES[g]
-            norm_grouped[g] = work.tile([P, GROUP, PACK], BF16, name="norm_grouped", align_bytes=64)
             copy(
-                out=norm_grouped[g][:, :tokens, :].rearrange("p (c i) t -> p c t i", i=4),
+                out=joint(g + 3)[:, :tokens, :].rearrange("p (c i) t -> p c t i", i=4),
                 in_=norm_planes[g][:, :, :tokens].rearrange("p t (c i) -> p c t i", i=4),
-            )
-
-        def quantise_norm(g):
-            norm_codes[g] = work.tile([P, GROUP], U32, name="norm_codes", align_bytes=64)
-            norm_scales[g] = work.tile([P, GROUP], U8, name="norm_scales", align_bytes=64)
-            tokens = P * SIZES[g]
-            nc.vector.quantize_mx(
-                out=norm_codes[g][:, :tokens].bitcast(FP8X4),
-                scales=norm_scales[g][:, :tokens],
-                in_=norm_grouped[g][:, :tokens, :].rearrange("p c t -> p (c t)"),
             )
 
         def second_matmul(g):
@@ -299,8 +307,8 @@ def tile_tsh_mid_block_pb_t_kernel(
                     j = first + jj
                     nc.tensor.matmul_mx(
                         out=head[g, a][:, jj, :],
-                        lhsT=norm_codes[g][:, j * P : (j + 1) * P].bitcast(FP8X4),
-                        lhsT_scale=norm_scales[g][:, j * P : (j + 1) * P],
+                        lhsT=codes[g + 3][:, j * P : (j + 1) * P].bitcast(FP8X4),
+                        lhsT_scale=scales[g + 3][:, j * P : (j + 1) * P],
                         rhs=wh_words[:].bitcast(FP8X4),
                         rhs_scale=wh_plane[:],
                         start=True,
@@ -329,18 +337,20 @@ def tile_tsh_mid_block_pb_t_kernel(
         transpose_h(0)
         copy_h(0, 0)
         spread_biases()
-        quantise_h(0)
+        quantise(-1)
         add_bias(0, 0)
-        first_matmul(0, 0)
-        first_matmul(0, 1)
+        run(first_matmul, 0, 0)
+        run(first_matmul, 0, 1)
         transpose_h(1)
         copy_h(1, 0)
         copy_h(1, 1)
         transpose_h(2)
-        residual_add(0, 0)
-        residual_add(0, 1)
-        squares(0, 0)
-        squares(0, 1)
+        run(residual_add, 0, 0)
+        run(residual_add, 0, 1)
+        run(squares, 0, 0)
+        run(squares, 0, 1)
+        add_bias(1, 0)
+        add_bias_on_gpsimd(1)
         nc.gpsimd.tensor_copy(out=gain[:], in_=gain_bf[:])
         nc.gpsimd.tensor_copy(out=shift[:], in_=shift_bf[:])
 
@@ -348,8 +358,8 @@ def tile_tsh_mid_block_pb_t_kernel(
         for r in range(LAST):
             run(load, r + 5)
             if r > 0:
+                run(add_bias, r + 1, 0)
                 run(residual_add, r, 0)
-            run(add_bias, r + 1, 0)
             run(copy_h, r + 2, 0)
             run(copy_h, r + 2, 1)
             run(transpose_x, r - 2, 0)
@@ -368,8 +378,7 @@ def tile_tsh_mid_block_pb_t_kernel(
             if r > 0:
                 run(squares, r, 0)
             run(gain_shift, r - 2, 3)
-            run(quantise_norm, r - 3)
-            run(quantise_h, r + 1)
+            quantise(r)
             run(second_matmul, r - 3)
             run(residual_add, r, 2)
             run(add_bias, r + 1, 1)
@@ -378,59 +387,54 @@ def tile_tsh_mid_block_pb_t_kernel(
             run(first_matmul, r + 1, 1)
             if r > 0:
                 run(squares, r, 1)
-            if r < LAST - 1:
-                run(regroup_on_scalar, r - 2)
+            run(regroup_on_scalar, r - 2)
             run(squares, r, 2)
             run(squares, r, 3)
             run(normalise, r - 1)
-            if r < LAST - 1:
-                run(regroup_on_gpsimd, r - 2)
+            run(regroup_on_gpsimd, r - 2)
+            if r > 0:
+                run(add_bias_on_gpsimd, r + 1)
             run(finish, r - 3)
             run(transpose_h, r + 3)
 
-        residual_add(LAST, 0)
-        residual_add(LAST, 1)
-        regroup_alone(LAST - 3, nc.vector.tensor_copy)
-        quantise_norm(LAST - 3)
+        for j in range(SIZES[LAST]):
+            residual_add(LAST, j)
         std_dev(LAST - 1)
         mean(LAST - 1)
-        squares(LAST, 0)
-        squares(LAST, 1)
-        std_dev(LAST)
-        mean(LAST)
-        transpose_x(LAST - 2, 0)
-        transpose_x(LAST - 2, 1)
-        transpose_x(LAST - 2, 2)
         normalise(LAST - 1, nc.vector)
-        normalise(LAST, nc.vector)
+        for t in range(3):
+            transpose_x(LAST - 2, t)
         gain_shift(LAST - 2, 0)
         transpose_x(LAST - 2, 3)
-        second_matmul(LAST - 3)
         gain_shift(LAST - 2, 1)
-        transpose_x(LAST - 1, 0)
+        for j in range(SIZES[LAST]):
+            squares(LAST, j)
+        std_dev(LAST)
+        mean(LAST)
+        for t in range(3):
+            transpose_x(LAST - 1, t)
         gain_shift(LAST - 2, 2)
-        transpose_x(LAST - 1, 1)
         gain_shift(LAST - 2, 3)
-        transpose_x(LAST - 1, 2)
-        finish(LAST - 3)
-        regroup_alone(LAST - 2, nc.vector.tensor_copy)
-        quantise_norm(LAST - 2)
-        gain_shift(LAST - 1, 0)
+        quantise(LAST)
+        second_matmul(LAST - 3)
         transpose_x(LAST - 1, 3)
+        normalise(LAST, nc.vector)
+        for t in range(PACK):
+            gain_shift(LAST - 1, t)
         for t in range(PACK):
             transpose_x(LAST, t)
+        regroup_alone(LAST - 2, nc.vector.tensor_copy)
+        finish(LAST - 3)
+        quantise(LAST + 1)
         second_matmul(LAST - 2)
-        gain_shift(LAST - 1, 1)
-        gain_shift(LAST - 1, 2)
-        gain_shift(LAST - 1, 3)
-        regroup_alone(LAST - 1, nc.vector.tensor_copy)
-        quantise_norm(LAST - 1)
         for t in range(PACK):
             gain_shift(LAST, t)
+        regroup_alone(LAST - 1, nc.vector.tensor_copy)
+        quantise(LAST + 2)
         finish(LAST - 2)
         second_matmul(LAST - 1)
         regroup_alone(LAST, nc.scalar.copy)
-        quantise_norm(LAST)
+        quantise(LAST + 3)
         finish(LAST - 1)
         second_matmul(LAST)
         finish(LAST)

@@ -166,16 +166,12 @@ def tile_tsh_mid_block_pb_t_kernel(
                         in_=grouped[c][:, lo:hi, :].rearrange("p c t -> p (c t)"),
                     )
 
-        def add_bias(g, a):
-            if a == 0:
-                res_bias[g] = work.tile([P, TILES, MID], F32, name="res_bias")
-            first = 2 * a
-            count = min(first + 2, SIZES[g] - GPSIMD_ADDS[g]) - first
-            if count <= 0:
-                return
+        def add_bias(g):
+            res_bias[g] = work.tile([P, TILES, MID], F32, name="res_bias")
+            count = SIZES[g] - GPSIMD_ADDS[g]
             nc.vector.tensor_tensor(
-                out=res_bias[g][:, first : first + count, :],
-                in0=res_sb[g][:, first : first + count, :],
+                out=res_bias[g][:, :count, :],
+                in0=res_sb[g][:, :count, :],
                 in1=bf_bank[:].unsqueeze(1).to_broadcast([P, count, MID]),
                 op=ALU.add,
             )
@@ -338,7 +334,7 @@ def tile_tsh_mid_block_pb_t_kernel(
         copy_h(0, 0)
         spread_biases()
         quantise(-1)
-        add_bias(0, 0)
+        add_bias(0)
         run(first_matmul, 0, 0)
         run(first_matmul, 0, 1)
         transpose_h(1)
@@ -349,7 +345,7 @@ def tile_tsh_mid_block_pb_t_kernel(
         run(residual_add, 0, 1)
         run(squares, 0, 0)
         run(squares, 0, 1)
-        add_bias(1, 0)
+        add_bias(1)
         add_bias_on_gpsimd(1)
         nc.gpsimd.tensor_copy(out=gain[:], in_=gain_bf[:])
         nc.gpsimd.tensor_copy(out=shift[:], in_=shift_bf[:])
@@ -358,7 +354,7 @@ def tile_tsh_mid_block_pb_t_kernel(
         for r in range(LAST):
             run(load, r + 5)
             if r > 0:
-                run(add_bias, r + 1, 0)
+                run(add_bias, r + 1)
                 run(residual_add, r, 0)
             run(copy_h, r + 2, 0)
             run(copy_h, r + 2, 1)
@@ -381,7 +377,6 @@ def tile_tsh_mid_block_pb_t_kernel(
             quantise(r)
             run(second_matmul, r - 3)
             run(residual_add, r, 2)
-            run(add_bias, r + 1, 1)
             run(first_matmul, r + 1, 0)
             run(residual_add, r, 3)
             run(first_matmul, r + 1, 1)

@@ -23,9 +23,10 @@ SIZES = [2] + [TILES] * 15 + [2]
 GROUPS = len(SIZES)
 FIRST_TOKEN = [P * sum(SIZES[:g]) for g in range(GROUPS)]
 assert P * sum(SIZES) == TOKENS
-SCALAR_SHARE = 64
+SCALAR_SHARE = 52
 
 GPSIMD_ADDS = [0, 2, 1, 0] + [0] * (GROUPS - 4)
+TENSOR_ADDS = [int(2 < g < GROUPS - 1 and g % 3 == 0) for g in range(GROUPS)]
 
 FLOPS = 2 * TOKENS * (FFN * MID + MID * D_OUT)
 
@@ -99,12 +100,14 @@ def tile_tsh_mid_block_pb_t_kernel(
         load_res(0)
         wf_words, wf_plane = load_weight(nc, consts, w_f2_words, w_f2_scales, MID, "wf")
         load(1)
-        load_h(2)
+        load(2)
+        load_h(3)
         wh_words, wh_plane = load_weight(nc, consts, w_h_words, w_h_scales, D_OUT, "wh")
-        load_res(2)
 
         ident = consts.tile([P, P], F32)
         make_identity(nc, ident[:])
+        ident_bf = consts.tile([P, P], BF16)
+        make_identity(nc, ident_bf[:])
         ones = consts.tile([P, P], BF16)
         nc.vector.memset(ones[:], 1.0)
         bf_rows = consts.tile([P, MID], BF16)
@@ -168,7 +171,7 @@ def tile_tsh_mid_block_pb_t_kernel(
 
         def add_bias(g):
             res_bias[g] = work.tile([P, TILES, MID], F32, name="res_bias")
-            count = SIZES[g] - GPSIMD_ADDS[g]
+            count = SIZES[g] - GPSIMD_ADDS[g] - TENSOR_ADDS[g]
             nc.vector.tensor_tensor(
                 out=res_bias[g][:, :count, :],
                 in0=res_sb[g][:, :count, :],
@@ -181,6 +184,13 @@ def tile_tsh_mid_block_pb_t_kernel(
                 nc.gpsimd.tensor_tensor(
                     out=res_bias[g][:, j, :], in0=res_sb[g][:, j, :], in1=bf_rows[:], op=ALU.add
                 )
+
+        def add_bias_on_tensor(g):
+            for j in range(SIZES[g] - TENSOR_ADDS[g], SIZES[g]):
+                bank = psum.tile([P, MID], F32, name="res_bank", tag="ffn", bufs=2)
+                nc.tensor.matmul(out=bank[:], lhsT=ident_bf[:], rhs=res_sb[g][:, j, :], start=True, stop=False)
+                nc.tensor.matmul(out=bank[:], lhsT=ones[:], rhs=bias_row[:, :MID], start=False, stop=True)
+                nc.scalar.copy(out=res_bias[g][:, j, :], in_=bank[:])
 
         def first_matmul(g, j):
             ffn[g, j] = psum.tile([P, MID], F32, name="ffn", tag="ffn", bufs=2)
@@ -328,7 +338,7 @@ def tile_tsh_mid_block_pb_t_kernel(
 
         by_tile = (first_matmul, residual_add, squares)
 
-        load(3)
+        load_res(3)
         load(4)
         transpose_h(0)
         copy_h(0, 0)
@@ -377,12 +387,17 @@ def tile_tsh_mid_block_pb_t_kernel(
             quantise(r)
             run(second_matmul, r - 3)
             run(residual_add, r, 2)
-            run(first_matmul, r + 1, 0)
+            if not TENSOR_ADDS[r + 1]:
+                run(first_matmul, r + 1, 0)
             run(residual_add, r, 3)
-            run(first_matmul, r + 1, 1)
+            if not TENSOR_ADDS[r + 1]:
+                run(first_matmul, r + 1, 1)
             if r > 0:
                 run(squares, r, 1)
             run(regroup_on_scalar, r - 2)
+            run(add_bias_on_tensor, r + 1)
+            if TENSOR_ADDS[r + 1]:
+                run(first_matmul, r + 1, 0)
             run(squares, r, 2)
             run(squares, r, 3)
             run(normalise, r - 1)
@@ -391,6 +406,8 @@ def tile_tsh_mid_block_pb_t_kernel(
                 run(add_bias_on_gpsimd, r + 1)
             run(finish, r - 3)
             run(transpose_h, r + 3)
+            if TENSOR_ADDS[r + 1]:
+                run(first_matmul, r + 1, 1)
 
         for j in range(SIZES[LAST]):
             residual_add(LAST, j)

@@ -377,12 +377,12 @@ def tile_tsh_mid_block_pb_t_kernel(
             run(first_matmul, r, 2)
             run(first_matmul, r, 3)
             run(transpose_x, r - 2, 3)
-            run(gain_shift, r - 2, 1)
-            run(std_dev, r - 1)
-            run(mean, r - 1)
-            run(gain_shift, r - 2, 2)
             if r > 0:
                 run(squares, r, 0)
+            run(std_dev, r - 1)
+            run(mean, r - 1)
+            run(gain_shift, r - 2, 1)
+            run(gain_shift, r - 2, 2)
             run(gain_shift, r - 2, 3)
             quantise(r)
             run(second_matmul, r - 3)

import concourse.mybir as mybir
from concourse.masks import make_identity

F32 = mybir.dt.float32
BF16 = mybir.dt.bfloat16
I32 = mybir.dt.int32
U32 = mybir.dt.uint32
U8 = mybir.dt.uint8
FP8X4 = mybir.dt.float8_e4m3fn_x4
ALU = mybir.AluOpType
ACT = mybir.ActivationFunctionType

P = 128
PACK = 4
TOKENS = 8 * 1024
FFN = 512
MID = 512
D_OUT = 256
LN_EPS = 1e-5
TILES = 4
GROUP = P * TILES
SIZES = [2] + [TILES] * 15 + [2]
GROUPS = len(SIZES)
FIRST_TOKEN = [P * sum(SIZES[:g]) for g in range(GROUPS)]
assert P * sum(SIZES) == TOKENS
SCALAR_SHARE = 52

GPSIMD_ADDS = [0, 2, 1, 0] + [0] * (GROUPS - 4)
TENSOR_ADDS = [int(2 < g < GROUPS - 1 and g % 3 == 0) for g in range(GROUPS)]

FLOPS = 2 * TOKENS * (FFN * MID + MID * D_OUT)


def load_weight(nc, consts, words_dram, scales_dram, width, name):
    words = consts.tile([P, width * PACK], U8, name=name + "_words", align_bytes=64)
    nc.sync.dma_start(
        out=words[:].bitcast(I32),
        in_=words_dram[0].rearrange("p n t -> p (n t)").bitcast(I32),
    )
    plane = consts.tile([P, width], U8, name=name + "_plane", align_bytes=64)
    nc.vector.memset(plane[:].bitcast(I32), 0)
    for r in range(4):
        nc.sync.dma_start(
            out=plane[r:P:32, :].bitcast(I32),
            in_=scales_dram[0, r:16:4, :].bitcast(I32),
        )
    return words, plane


def tile_tsh_mid_block_pb_t_kernel(
    tc, h, w_f2_words, w_f2_scales, b_f2, res1, g2, be2, w_h_words, w_h_scales, b_h, out
):
    nc = tc.nc

    def by_group(rows):
        return [
            rows[FIRST_TOKEN[g] : FIRST_TOKEN[g] + P * SIZES[g], :].rearrange("(p j) k -> p j k", j=SIZES[g])
            for g in range(GROUPS)
        ]

    h_groups = by_group(h.flatten_outer_dims())
    res_groups = by_group(res1.flatten_outer_dims())
    out_groups = by_group(out.flatten_outer_dims())

    def pairs(g):
        return [(a, 2 * a, min(2, SIZES[g] - 2 * a)) for a in range((SIZES[g] + 1) // 2)]

    with tc.tile_pool(name="consts", bufs=1) as consts, tc.tile_pool(name="loads", bufs=5) as loads, tc.tile_pool(
        name="work", bufs=2
    ) as work, tc.tile_pool(name="stats", bufs=4) as stats, tc.psum_pool(
        name="psum", bufs=1
    ) as psum, tc.manual_schedule():
        h_sb, res_sb, hT, grouped, codes, scales, res_bias, ffn = {}, {}, {}, {}, {}, {}, {}, {}
        x, row_sum, sq_sum, neg_mean, rstd, std, x_hat, xT = {}, {}, {}, {}, {}, {}, {}, {}
        norm_planes, head = {}, {}

        def load_h(g):
            h_sb[g] = loads.tile([P, TILES, FFN], BF16, name="h_sb")
            nc.sync.dma_start(out=h_sb[g][:, : SIZES[g], :], in_=h_groups[g])

        def load_res(g):
            res_sb[g] = loads.tile([P, TILES, MID], BF16, name="res_sb")
            nc.sync.dma_start(out=res_sb[g][:, : SIZES[g], :], in_=res_groups[g])

        def load(g):
            load_h(g)
            load_res(g)

        eps_col = consts.tile([P, 1], F32)
        nc.vector.memset(eps_col[:], LN_EPS)
        warm = consts.tile([P, 1], F32)
        nc.scalar.activation(out=warm[:], in_=eps_col[:], func=ACT.Abs_reciprocal_sqrt)

        bias_row = consts.tile([P, MID + D_OUT], BF16)
        nc.vector.memset(bias_row[:], 0.0)
        nc.scalar.dma_start(out=bias_row[0:1, :MID], in_=b_f2.unsqueeze(0))
        nc.scalar.dma_start(out=bias_row[0:1, MID:], in_=b_h.unsqueeze(0))

        load_h(0)
        load_res(0)
        wf_words, wf_plane = load_weight(nc, consts, w_f2_words, w_f2_scales, MID, "wf")
        load(1)
        load(2)
        load_h(3)
        wh_words, wh_plane = load_weight(nc, consts, w_h_words, w_h_scales, D_OUT, "wh")

        ident = consts.tile([P, P], F32)
        make_identity(nc, ident[:])
        ident_bf = consts.tile([P, P], BF16)
        make_identity(nc, ident_bf[:])
        ones = consts.tile([P, P], BF16)
        nc.vector.memset(ones[:], 1.0)
        bf_rows = consts.tile([P, MID], BF16)
        bh_rows = consts.tile([P, D_OUT], BF16)
        bf_bank = psum.tile([P, MID], F32, name="bf_bank", tag="bf_bank", bufs=1)

        def spread_biases():
            nc.tensor.matmul(out=bf_bank[:], lhsT=ones[:], rhs=bias_row[:, :MID], start=True, stop=True)
            bank = psum.tile([P, GROUP], F32, name="bank", tag="xT", bufs=3)
            nc.tensor.matmul(out=bank[:, :D_OUT], lhsT=ones[:], rhs=bias_row[:, MID:], start=True, stop=True)
            nc.scalar.copy(out=bh_rows[:], in_=bank[:, :D_OUT])
            nc.scalar.copy(out=bf_rows[:], in_=bf_bank[:])

        gain_bf = consts.tile([P, PACK], BF16)
        nc.sync.dma_start(out=gain_bf[:], in_=g2.rearrange("(p t) -> p t", t=PACK))
        shift_bf = consts.tile([P, PACK], BF16)
        nc.sync.dma_start(out=shift_bf[:], in_=be2.rearrange("(p t) -> p t", t=PACK))
        gain = consts.tile([P, PACK], F32)
        shift = consts.tile([P, PACK], F32)

        def transpose_h(g):
            h_words = h_sb[g][:].bitcast(F32)
            for a, first, count in pairs(g):
                hT[g, a] = psum.tile([P, 2, 2 * P], F32, name="hT", tag="short", bufs=2)
                for jj in range(count):
                    for u in range(2):
                        nc.tensor.transpose(
                            out=hT[g, a][:, u, jj * P : (jj + 1) * P],
                            in_=h_words[:, first + jj, u : FFN // 2 : 2],
                            identity=ident[:],
                        )

        def joint(c):
            if c not in grouped:
                grouped[c] = work.tile([P, 2 * GROUP, PACK], BF16, name="grouped", align_bytes=64, bufs=4)
            return grouped[c]

        def copy_h(g, a):
            if a >= len(pairs(g)):
                return
            first, count = pairs(g)[a][1:]
            words = joint(g - 1)[:, GROUP:, :].rearrange("p c t -> p (c t)").bitcast(F32).rearrange("p (c u) -> p c u", u=2)
            nc.scalar.copy(
                out=words[:, first * P : (first + count) * P, :],
                in_=hT[g, a][:, :, : count * P].rearrange("p u c -> p c u"),
            )

        def quantise(c):
            codes[c] = work.tile([P, 2 * GROUP], U32, name="codes", align_bytes=64, bufs=4)
            scales[c] = work.tile([P, 2 * GROUP], U8, name="scales", align_bytes=64, bufs=4)
            norm = P * SIZES[c - 3] if 0 <= c - 3 < GROUPS else 0
            h_end = GROUP + (P * SIZES[c + 1] if c + 1 < GROUPS else 0)
            spans = [(0, 2 * GROUP)] if (norm, h_end) == (GROUP, 2 * GROUP) else [(0, norm), (GROUP, h_end)]
            for lo, hi in spans:
                if lo < hi:
                    nc.vector.quantize_mx(
                        out=codes[c][:, lo:hi].bitcast(FP8X4),
                        scales=scales[c][:, lo:hi],
                        in_=grouped[c][:, lo:hi, :].rearrange("p c t -> p (c t)"),
                    )

        def add_bias(g):
            res_bias[g] = work.tile([P, TILES, MID], F32, name="res_bias")
            count = SIZES[g] - GPSIMD_ADDS[g] - TENSOR_ADDS[g]
            nc.vector.tensor_tensor(
                out=res_bias[g][:, :count, :],
                in0=res_sb[g][:, :count, :],
                in1=bf_bank[:].unsqueeze(1).to_broadcast([P, count, MID]),
                op=ALU.add,
            )

        def add_bias_on_gpsimd(g):
            for j in range(SIZES[g] - GPSIMD_ADDS[g], SIZES[g]):
                nc.gpsimd.tensor_tensor(
                    out=res_bias[g][:, j, :], in0=res_sb[g][:, j, :], in1=bf_rows[:], op=ALU.add
                )

        def add_bias_on_tensor(g):
            for j in range(SIZES[g] - TENSOR_ADDS[g], SIZES[g]):
                bank = psum.tile([P, MID], F32, name="res_bank", tag="ffn", bufs=2)
                nc.tensor.matmul(out=bank[:], lhsT=ident_bf[:], rhs=res_sb[g][:, j, :], start=True, stop=False)
                nc.tensor.matmul(out=bank[:], lhsT=ones[:], rhs=bias_row[:, :MID], start=False, stop=True)
                nc.scalar.copy(out=res_bias[g][:, j, :], in_=bank[:])

        def first_matmul(g, j):
            ffn[g, j] = psum.tile([P, MID], F32, name="ffn", tag="ffn", bufs=2)
            nc.tensor.matmul_mx(
                out=ffn[g, j][:],
                lhsT=codes[g - 1][:, GROUP + j * P : GROUP + (j + 1) * P].bitcast(FP8X4),
                lhsT_scale=scales[g - 1][:, GROUP + j * P : GROUP + (j + 1) * P],
                rhs=wf_words[:].bitcast(FP8X4),
                rhs_scale=wf_plane[:],
                start=True,
                stop=True,
            )

        def residual_add(g, j):
            if j == 0:
                x[g] = work.tile([P, TILES, MID], F32, name="x", bufs=3)
                row_sum[g] = stats.tile([P, TILES], F32, name="row_sum")
            nc.vector.scalar_tensor_tensor(
                out=x[g][:, j, :],
                in0=ffn[g, j][:],
                scalar=0.0,
                in1=res_bias[g][:, j, :],
                op0=ALU.add,
                op1=ALU.add,
                accum_out=row_sum[g][:, j : j + 1],
            )

        def squares(g, j):
            if j == 0:
                sq_sum[g] = stats.tile([P, TILES], F32, name="sq_sum")
            junk = work.tile([P, MID], BF16, name="junk")
            nc.scalar.activation(
                out=junk[:],
                in_=x[g][:, j, :],
                func=ACT.Square,
                bias=row_sum[g][:, j : j + 1],
                scale=-float(MID),
                accum_out=sq_sum[g][:, j : j + 1],
            )

        def std_dev(g):
            rstd[g] = stats.tile([P, TILES], F32, name="rstd")
            nc.scalar.activation(
                out=rstd[g][:, : SIZES[g]],
                in_=sq_sum[g][:, : SIZES[g]],
                func=ACT.Abs_reciprocal_sqrt,
                bias=eps_col[:, 0:1],
                scale=1.0 / MID**3,
            )

        def mean(g):
            neg_mean[g] = stats.tile([P, TILES], F32, name="neg_mean")
            nc.scalar.mul(out=neg_mean[g][:, : SIZES[g]], in_=row_sum[g][:, : SIZES[g]], mul=-1.0 / MID)

        def normalise(g, engine=nc.gpsimd):
            x_hat[g] = work.tile([P, TILES, MID], F32, name="x_hat", bufs=3)
            for j in range(SIZES[g]):
                engine.tensor_scalar(
                    out=x_hat[g][:, j, :],
                    in0=x[g][:, j, :],
                    scalar1=neg_mean[g][:, j : j + 1],
                    scalar2=rstd[g][:, j : j + 1],
                    op0=ALU.add,
                    op1=ALU.mult,
                )

        def transpose_x(g, t):
            if g == GROUPS - 2 and t < 2:
                xT[g, t] = psum.tile([P, GROUP], F32, name="xT_late", tag="ffn", bufs=2)
            elif g < GROUPS - 1:
                xT[g, t] = psum.tile([P, GROUP], F32, name="xT", tag="xT", bufs=3)
            elif t % 2 == 0:
                both = psum.tile([P, GROUP], F32, name="both", tag="xT", bufs=3)
                xT[g, t], xT[g, t + 1] = both[:, : GROUP // 2], both[:, GROUP // 2 :]
            for j in range(SIZES[g]):
                nc.tensor.transpose(
                    out=xT[g, t][:, j * P : (j + 1) * P], in_=x_hat[g][:, j, t:MID:PACK], identity=ident[:]
                )

        def gain_shift(g, t):
            if t == 0:
                norm_planes[g] = work.tile([P, PACK, GROUP], BF16, name="norm_planes", bufs=3)
            nc.scalar.activation(
                out=norm_planes[g][:, t, : P * SIZES[g]],
                in_=xT[g, t][:, : P * SIZES[g]],
                func=ACT.Identity,
                bias=shift[:, t : t + 1],
                scale=gain[:, t : t + 1],
            )

        def regroup_on_scalar(g):
            share = SCALAR_SHARE * SIZES[g]
            nc.scalar.copy(
                out=joint(g + 3)[:, :share, :].rearrange("p (c i) t -> p c t i", i=4),
                in_=norm_planes[g][:, :, :share].rearrange("p t (c i) -> p c t i", i=4),
            )

        def regroup_on_gpsimd(g):
            share, tokens = SCALAR_SHARE * SIZES[g], P * SIZES[g]
            nc.gpsimd.tensor_scalar(
                out=joint(g + 3)[:, share:tokens, :],
                in0=norm_planes[g][:, :, share:tokens].rearrange("p t n -> p n t"),
                scalar1=1.0,
                scalar2=0.0,
                op0=ALU.mult,
                op1=ALU.add,
            )

        def regroup_alone(g, copy):
            tokens = P * SIZES[g]
            copy(
                out=joint(g + 3)[:, :tokens, :].rearrange("p (c i) t -> p c t i", i=4),
                in_=norm_planes[g][:, :, :tokens].rearrange("p t (c i) -> p c t i", i=4),
            )

        def second_matmul(g):
            for a, first, count in pairs(g):
                head[g, a] = psum.tile([P, 2, D_OUT], F32, name="head", tag="short", bufs=2)
                for jj in range(count):
                    j = first + jj
                    nc.tensor.matmul_mx(
                        out=head[g, a][:, jj, :],
                        lhsT=codes[g + 3][:, j * P : (j + 1) * P].bitcast(FP8X4),
                        lhsT_scale=scales[g + 3][:, j * P : (j + 1) * P],
                        rhs=wh_words[:].bitcast(FP8X4),
                        rhs_scale=wh_plane[:],
                        start=True,
                        stop=True,
                    )

        def finish(g):
            result = work.tile([P, TILES, D_OUT], F32, name="result", bufs=3)
            for a, first, count in pairs(g):
                nc.vector.tensor_tensor(
                    out=result[:, first : first + count, :],
                    in0=head[g, a][:, :count, :],
                    in1=bh_rows[:].unsqueeze(1).to_broadcast([P, count, D_OUT]),
                    op=ALU.add,
                )
                nc.sync.dma_start(out=out_groups[g][:, first : first + count, :], in_=result[:, first : first + count, :])

        def run(stage, g, *which):
            if 0 <= g < GROUPS and not (stage in by_tile and which[0] >= SIZES[g]):
                stage(g, *which)

        by_tile = (first_matmul, residual_add, squares)

        load_res(3)
        load(4)
        transpose_h(0)
        copy_h(0, 0)
        spread_biases()
        quantise(-1)
        add_bias(0)
        run(first_matmul, 0, 0)
        run(first_matmul, 0, 1)
        transpose_h(1)
        copy_h(1, 0)
        copy_h(1, 1)
        transpose_h(2)
        run(residual_add, 0, 0)
        run(residual_add, 0, 1)
        run(squares, 0, 0)
        run(squares, 0, 1)
        add_bias(1)
        add_bias_on_gpsimd(1)
        nc.gpsimd.tensor_copy(out=gain[:], in_=gain_bf[:])
        nc.gpsimd.tensor_copy(out=shift[:], in_=shift_bf[:])

        LAST = GROUPS - 1
        for r in range(LAST):
            run(load, r + 5)
            if r > 0:
                run(add_bias, r + 1)
                run(residual_add, r, 0)
            run(copy_h, r + 2, 0)
            run(copy_h, r + 2, 1)
            run(transpose_x, r - 2, 0)
            run(transpose_x, r - 2, 1)
            run(transpose_x, r - 2, 2)
            if r > 0:
                run(residual_add, r, 1)
            run(gain_shift, r - 2, 0)
            run(first_matmul, r, 2)
            run(first_matmul, r, 3)
            run(transpose_x, r - 2, 3)
            if r > 0:
                run(squares, r, 0)
            run(std_dev, r - 1)
            run(mean, r - 1)
            run(gain_shift, r - 2, 1)
            run(gain_shift, r - 2, 2)
            run(gain_shift, r - 2, 3)
            quantise(r)
            run(second_matmul, r - 3)
            run(residual_add, r, 2)
            if not TENSOR_ADDS[r + 1]:
                run(first_matmul, r + 1, 0)
            run(residual_add, r, 3)
            if not TENSOR_ADDS[r + 1]:
                run(first_matmul, r + 1, 1)
            if r > 0:
                run(squares, r, 1)
            run(regroup_on_scalar, r - 2)
            run(add_bias_on_tensor, r + 1)
            if TENSOR_ADDS[r + 1]:
                run(first_matmul, r + 1, 0)
            run(squares, r, 2)
            run(squares, r, 3)
            run(normalise, r - 1)
            run(regroup_on_gpsimd, r - 2)
            if r > 0:
                run(add_bias_on_gpsimd, r + 1)
            run(finish, r - 3)
            run(transpose_h, r + 3)
            if TENSOR_ADDS[r + 1]:
                run(first_matmul, r + 1, 1)

        for j in range(SIZES[LAST]):
            residual_add(LAST, j)
        std_dev(LAST - 1)
        mean(LAST - 1)
        normalise(LAST - 1, nc.vector)
        for t in range(3):
            transpose_x(LAST - 2, t)
        gain_shift(LAST - 2, 0)
        transpose_x(LAST - 2, 3)
        gain_shift(LAST - 2, 1)
        for j in range(SIZES[LAST]):
            squares(LAST, j)
        std_dev(LAST)
        mean(LAST)
        for t in range(3):
            transpose_x(LAST - 1, t)
        gain_shift(LAST - 2, 2)
        gain_shift(LAST - 2, 3)
        quantise(LAST)
        second_matmul(LAST - 3)
        transpose_x(LAST - 1, 3)
        normalise(LAST, nc.vector)
        for t in range(PACK):
            gain_shift(LAST - 1, t)
        for t in range(PACK):
            transpose_x(LAST, t)
        regroup_alone(LAST - 2, nc.vector.tensor_copy)
        finish(LAST - 3)
        quantise(LAST + 1)
        second_matmul(LAST - 2)
        for t in range(PACK):
            gain_shift(LAST, t)
        regroup_alone(LAST - 1, nc.vector.tensor_copy)
        quantise(LAST + 2)
        finish(LAST - 2)
        second_matmul(LAST - 1)
        regroup_alone(LAST, nc.scalar.copy)
        quantise(LAST + 3)
        finish(LAST - 1)
        second_matmul(LAST)
        finish(LAST)
